import numpy as np
import ml_dtypes


def mxq(x, axis, fmt="e4m3"):
    dtype, down = {"e4m3": (ml_dtypes.float8_e4m3fn, 7), "e5m2": (ml_dtypes.float8_e5m2, 14)}[fmt]
    v = np.moveaxis(np.asarray(x, np.float32).astype(ml_dtypes.bfloat16).astype(np.float64), axis, -1)
    blocks = v.reshape(v.shape[:-1] + (-1, 32))
    amax = np.abs(blocks).max(-1, keepdims=True)
    byte = np.maximum(np.where(amax > 0, np.frexp(amax)[1] - 1 + 127, 0) - down, 1)
    scale = np.exp2(byte - 127.0)
    codes = (blocks / scale).astype(np.float32).astype(dtype).astype(np.float64)
    return np.moveaxis((codes * scale).reshape(v.shape), -1, axis)


WIDE = False


def mx_kscale(k):
    if not WIDE:
        return np.ones(k)
    levels = np.array([10, -10, 5, -5, 0])
    if k % 512:
        return np.exp2(np.random.permutation(np.resize(levels, k // 32))).repeat(32)
    a = np.empty((k // 512, 16))
    for p in range(k // 512):
        a[p, :8] = np.random.permutation(np.resize(levels, 8))
        for g in range(8):
            far = levels[np.abs(levels - a[p, g]) >= 10]
            a[p, g + 8] = far[np.random.randint(len(far))]
    return np.exp2(a.ravel()).repeat(32)


BF16 = ml_dtypes.bfloat16


def bf(x):
    return np.asarray(x, np.float32).astype(BF16)


def f64(x):
    return np.asarray(x).astype(np.float64)


B, T, E, H, C, W = 1, 1024, 1024, 8, 250, 256
D = E // H
MAX_PERIOD = 10000.0


def rope_tables():
    freqs = np.exp(np.arange(D // 2, dtype=np.float64) * (-np.log(MAX_PERIOD) * 2.0 / D))
    ang = np.arange(T, dtype=np.float64)[:, None] * freqs[None, :]
    return np.cos(ang), np.sin(ang)


def rot(x, cos, sin):
    xr = x.reshape(B, H, T, D // 2, 2)
    xa, xb = xr[..., 0], xr[..., 1]
    ya = xa * cos - xb * sin
    yb = xa * sin + xb * cos
    return np.stack([ya, yb], axis=-1).reshape(B, H, T, D)


def setup_inputs():
    s = mx_kscale(E)
    return {"query": bf(np.random.standard_normal((B, T, E)) * s),
            "in_proj_w": bf(np.random.standard_normal((3 * E, E)) / np.sqrt(E) / s[None, :])}


def reference(query, in_proj_w):
    proj = mxq(f64(query), 2, "e4m3") @ mxq(f64(in_proj_w), 1, "e4m3").T
    qkv = proj.reshape(B, T, 3, H, D)
    q = qkv[:, :, 0].transpose(0, 2, 1, 3)
    k = qkv[:, :, 1].transpose(0, 2, 1, 3)
    v = qkv[:, :, 2].transpose(0, 2, 1, 3)
    cos, sin = rope_tables()
    return rot(q, cos, sin), rot(k, cos, sin), v

@@ -1,0 +1,285 @@
+import math
+from contextlib import ExitStack
+
+import concourse.mybir as mybir
+from concourse.masks import make_identity
+
+F32 = mybir.dt.float32
+BF16 = mybir.dt.bfloat16
+I32 = mybir.dt.int32
+U32 = mybir.dt.uint32
+U8 = mybir.dt.uint8
+FP8X4 = mybir.dt.float8_e4m3fn_x4
+ALU = mybir.AluOpType
+ACT = mybir.ActivationFunctionType
+
+P = 128
+T = 1024
+E = 1024
+HEAD = 128
+PAIRS = HEAD // 2
+K_PASS = 4 * P
+PASSES = E // K_PASS
+WORDS = E // 2
+T_BLOCKS = T // P
+ROUNDS = 4
+QK_COLS = 512
+V_COLS = 256
+QK_HEADS = QK_COLS // HEAD
+V_HEADS = V_COLS // HEAD
+ROW_BLOCKS = (QK_COLS + V_COLS) // P
+STORE_BLOCKS = 4
+FIRST_BUNCH_AT = 2
+SECOND_BUNCH_AT = 5
+
+FLOPS = 2 * T * E * 3 * E
+
+FREQ_RATIO = math.exp(-math.log(10000.0) * 2.0 / HEAD)
+TWO_PI = 2.0 * math.pi
+ROUND_MAGIC = 1.5 * 2.0**23
+TWO_PI_HIGH = 6.28125
+TWO_PI_REST = TWO_PI - TWO_PI_HIGH
+
+
+def tile_mimistreamingmultiheadattention_pa_kernel(tc, query, in_proj_w, out_0, out_1, out_2):
+    nc = tc.nc
+    with ExitStack() as ctx:
+        const = ctx.enter_context(tc.tile_pool(name="const", bufs=1))
+        scratch = ctx.enter_context(tc.tile_pool(name="scratch", bufs=1))
+        loads = ctx.enter_context(tc.tile_pool(name="loads", bufs=1))
+        grouped_pool = ctx.enter_context(tc.tile_pool(name="grouped", bufs=2))
+        mx = ctx.enter_context(tc.tile_pool(name="mx", bufs=1))
+        work = ctx.enter_context(tc.tile_pool(name="work", bufs=3))
+        stage = ctx.enter_context(tc.tile_pool(name="stage", bufs=4))
+        tp_pool = ctx.enter_context(tc.psum_pool(name="tp", bufs=3))
+        acc_pool = ctx.enter_context(tc.psum_pool(name="acc", bufs=3))
+        accv_pool = ctx.enter_context(tc.psum_pool(name="accv", bufs=2))
+
+        q_sb = loads.tile([P, T_BLOCKS, E], BF16)
+        q_rows = query.rearrange("b (p i) k -> p (b i) k", i=T_BLOCKS)
+        w_sb = {}
+        for r in range(ROUNDS):
+            w_sb[r] = loads.tile([P, ROW_BLOCKS, E], BF16, name="w_sb%d" % r)
+
+        def load_query(pair):
+            nc.sync.dma_start(out=q_sb[:, 2 * pair : 2 * pair + 2, :], in_=q_rows[:, 2 * pair : 2 * pair + 2, :])
+
+        def load_weights(r, first_block, first_row):
+            rows = in_proj_w[first_row : first_row + 2 * P, :].rearrange("(b p) k -> p b k", p=P)
+            nc.sync.dma_start(out=w_sb[r][:, first_block : first_block + 2, :], in_=rows)
+
+        def load_round(r):
+            load_weights(r, 0, QK_COLS * r)
+            load_weights(r, 2, QK_COLS * r + 2 * P)
+            load_weights(r, 4, 2 * E + V_COLS * r)
+
+        load_weights(0, 0, 0)
+        load_weights(0, 2, 2 * P)
+        load_query(0)
+        load_weights(0, 4, 2 * E)
+        for pair in range(1, T_BLOCKS // 2):
+            load_query(pair)
+        for r in range(1, ROUNDS):
+            load_round(r)
+
+        ident = const.tile([P, P], F32)
+        make_identity(nc, ident[:])
+
+        pos_int = const.tile([P, T_BLOCKS], I32)
+        nc.gpsimd.iota(pos_int[:], pattern=[[1, T_BLOCKS]], base=0, channel_multiplier=T_BLOCKS)
+        pos = const.tile([P, T_BLOCKS], F32)
+        nc.vector.tensor_copy(out=pos[:], in_=pos_int[:])
+
+        freq = const.tile([P, PAIRS], F32)
+        nc.vector.memset(freq[:, 0:1], 1.0)
+        for doubling in range(6):
+            width = 2**doubling
+            nc.vector.tensor_scalar(
+                out=freq[:, width : 2 * width],
+                in0=freq[:, 0:width],
+                scalar1=FREQ_RATIO**width,
+                scalar2=None,
+                op0=ALU.mult,
+            )
+
+        table_shape = [P, T_BLOCKS, PAIRS]
+        angle = scratch.tile(table_shape, F32)
+        nc.vector.tensor_tensor(
+            out=angle[:],
+            in0=pos[:].unsqueeze(2).to_broadcast(table_shape),
+            in1=freq[:].unsqueeze(1).to_broadcast(table_shape),
+            op=ALU.mult,
+        )
+
+        def flat(tile_ap):
+            return tile_ap.rearrange("p i j -> p (i j)")
+
+        turns = scratch.tile(table_shape, F32)
+        nc.vector.tensor_scalar(
+            out=flat(turns[:]), in0=flat(angle[:]), scalar1=1.0 / TWO_PI, scalar2=ROUND_MAGIC, op0=ALU.mult, op1=ALU.add
+        )
+        whole = scratch.tile(table_shape, F32)
+        nc.vector.tensor_scalar(
+            out=flat(whole[:]), in0=flat(turns[:]), scalar1=ROUND_MAGIC, scalar2=-TWO_PI_HIGH, op0=ALU.subtract, op1=ALU.mult
+        )
+        rest_high = scratch.tile(table_shape, F32)
+        nc.vector.tensor_tensor(out=flat(rest_high[:]), in0=flat(angle[:]), in1=flat(whole[:]), op=ALU.add)
+        rest = scratch.tile(table_shape, F32)
+        nc.vector.scalar_tensor_tensor(
+            out=flat(rest[:]),
+            in0=flat(whole[:]),
+            scalar=TWO_PI_REST / TWO_PI_HIGH,
+            in1=flat(rest_high[:]),
+            op0=ALU.mult,
+            op1=ALU.add,
+        )
+
+        sin_half = scratch.tile(table_shape, F32)
+        nc.scalar.activation(out=flat(sin_half[:]), in_=flat(rest[:]), func=ACT.Sin, scale=0.5)
+        sin_quarter = scratch.tile(table_shape, F32)
+        nc.scalar.activation(out=flat(sin_quarter[:]), in_=flat(rest[:]), func=ACT.Sin, scale=0.25)
+        sq_half = scratch.tile(table_shape, F32)
+        nc.scalar.activation(out=flat(sq_half[:]), in_=flat(sin_half[:]), func=ACT.Square)
+        sq_quarter = scratch.tile(table_shape, F32)
+        nc.scalar.activation(out=flat(sq_quarter[:]), in_=flat(sin_quarter[:]), func=ACT.Square)
+
+        cos = const.tile(table_shape, F32)
+        nc.vector.tensor_scalar(
+            out=flat(cos[:]), in0=flat(sq_half[:]), scalar1=-2.0, scalar2=1.0, op0=ALU.mult, op1=ALU.add
+        )
+        twice_cos_half = scratch.tile(table_shape, F32)
+        nc.vector.tensor_scalar(
+            out=flat(twice_cos_half[:]), in0=flat(sq_quarter[:]), scalar1=-4.0, scalar2=2.0, op0=ALU.mult, op1=ALU.add
+        )
+        sin_pm = const.tile([P, T_BLOCKS, 2, PAIRS], F32)
+        nc.vector.scalar_tensor_tensor(
+            out=sin_pm[:, :, 0, :], in0=sin_half[:], scalar=-1.0, in1=twice_cos_half[:], op0=ALU.mult, op1=ALU.mult
+        )
+        nc.vector.tensor_tensor(out=sin_pm[:, :, 1, :], in0=sin_half[:], in1=twice_cos_half[:], op=ALU.mult)
+
+        def transpose_block(src_words, dst_words):
+            tp = tp_pool.tile([P, PASSES, 2, P], F32)
+            for g in range(PASSES):
+                for u in range(2):
+                    first = 2 * P * g + u
+                    nc.tensor.transpose(tp[:, g, u, :], src_words[:, first : 2 * P * (g + 1) : 2], ident[:])
+            nc.scalar.copy(out=dst_words, in_=tp[:].rearrange("p g u r -> p g r u"))
+
+        def quantise(grouped, codes, scales):
+            nc.vector.quantize_mx(
+                out=codes.rearrange("p g c -> p (g c)").bitcast(FP8X4),
+                scales=scales.rearrange("p g c -> p (g c)"),
+                in_=grouped.rearrange("p g c t -> p (g c t)"),
+            )
+
+        q_codes = mx.tile([P, T_BLOCKS // 2, PASSES, 2 * P], U32, align_bytes=64)
+        q_scales = mx.tile([P, T_BLOCKS // 2, PASSES, 2 * P], U8, align_bytes=64)
+
+        def prepare_query(pair):
+            q_grouped = grouped_pool.tile([P, PASSES, 2 * P, 4], BF16, align_bytes=64)
+            for half in range(2):
+                transpose_block(
+                    q_sb[:].bitcast(F32)[:, 2 * pair + half, :],
+                    q_grouped[:].bitcast(F32)[:, :, P * half : P * half + P, :],
+                )
+            quantise(q_grouped[:], q_codes[:, pair], q_scales[:, pair])
+
+        qk_grouped = {}
+        v_grouped = {}
+        qk_codes = {}
+        qk_scales = {}
+        v_codes = {}
+        v_scales = {}
+
+        def transpose_weights(r, blocks):
+            if r not in qk_grouped:
+                qk_grouped[r] = grouped_pool.tile([P, PASSES, QK_COLS, 4], BF16, tag="qk_grouped", name="qk_grouped%d" % r, align_bytes=64)
+                v_grouped[r] = grouped_pool.tile([P, PASSES, V_COLS, 4], BF16, tag="v_grouped", name="v_grouped%d" % r, align_bytes=64)
+            for b in blocks:
+                if b < QK_COLS // P:
+                    dst = qk_grouped[r][:].bitcast(F32)[:, :, P * b : P * b + P, :]
+                else:
+                    first = P * b - QK_COLS
+                    dst = v_grouped[r][:].bitcast(F32)[:, :, first : first + P, :]
+                transpose_block(w_sb[r][:].bitcast(F32)[:, b, :], dst)
+
+        def quantise_weights(r):
+            qk_codes[r] = mx.tile([P, PASSES, QK_COLS], U32, name="qk_codes%d" % r, align_bytes=64)
+            qk_scales[r] = mx.tile([P, PASSES, QK_COLS], U8, name="qk_scales%d" % r, align_bytes=64)
+            v_codes[r] = mx.tile([P, PASSES, V_COLS], U32, name="v_codes%d" % r, align_bytes=64)
+            v_scales[r] = mx.tile([P, PASSES, V_COLS], U8, name="v_scales%d" % r, align_bytes=64)
+            quantise(qk_grouped[r][:], qk_codes[r][:], qk_scales[r][:])
+            quantise(v_grouped[r][:], v_codes[r][:], v_scales[r][:])
+
+        def multiply(acc, i, codes, scales):
+            cols = slice(P * (i % 2), P * (i % 2) + P)
+            for g in range(PASSES):
+                nc.tensor.matmul_mx(
+                    out=acc,
+                    lhsT=q_codes[:, i // 2, g, cols].bitcast(FP8X4),
+                    lhsT_scale=q_scales[:, i // 2, g, cols],
+                    rhs=codes[:, g, :].bitcast(FP8X4),
+                    rhs_scale=scales[:, g, :],
+                    start=(g == 0),
+                    stop=(g == PASSES - 1),
+                )
+
+        out_views = [o.rearrange("b h (p i) d -> p (b h) i d", i=T_BLOCKS) for o in (out_0, out_1, out_2)]
+        staged = {}
+
+        def project_and_rotate(r, i):
+            slot = i % STORE_BLOCKS
+            if slot == 0:
+                staged["qk"] = stage.tile([P, QK_HEADS, STORE_BLOCKS, HEAD], F32, tag="qk_stage", name="qk_stage")
+                staged["v"] = stage.tile([P, V_HEADS, STORE_BLOCKS, HEAD], F32, tag="v_stage", name="v_stage")
+            qk_stage = staged["qk"]
+            v_stage = staged["v"]
+
+            acc = acc_pool.tile([P, QK_COLS], F32)
+            multiply(acc[:], i, qk_codes[r], qk_scales[r])
+            accv = accv_pool.tile([P, V_COLS], F32)
+            multiply(accv[:], i, v_codes[r], v_scales[r])
+
+            pair_shape = [P, QK_HEADS, PAIRS, 2]
+            with_cos = work.tile([P, QK_COLS], F32)
+            nc.vector.tensor_tensor(
+                out=with_cos[:].rearrange("p (h j e) -> p h j e", h=QK_HEADS, e=2),
+                in0=acc[:].rearrange("p (h j e) -> p h j e", h=QK_HEADS, e=2),
+                in1=cos[:, i, :].unsqueeze(1).unsqueeze(3).to_broadcast(pair_shape),
+                op=ALU.mult,
+            )
+            with_sin = work.tile([P, 2, QK_COLS // 2], F32)
+            by_parity = acc[:].rearrange("p (h j e) -> p e h j", h=QK_HEADS, e=2)
+            for e in range(2):
+                nc.vector.tensor_tensor(
+                    out=with_sin[:, e, :].rearrange("p (h j) -> p h j", h=QK_HEADS),
+                    in0=by_parity[:, 1 - e],
+                    in1=sin_pm[:, i, e, :].unsqueeze(1).to_broadcast([P, QK_HEADS, PAIRS]),
+                    op=ALU.mult,
+                )
+            nc.gpsimd.tensor_tensor(
+                out=qk_stage[:, :, slot, :].rearrange("p h (j e) -> p h j e", e=2),
+                in0=with_cos[:].rearrange("p (h j e) -> p h j e", h=QK_HEADS, e=2),
+                in1=with_sin[:].rearrange("p e (h j) -> p h j e", h=QK_HEADS),
+                op=ALU.add,
+            )
+            nc.scalar.copy(out=v_stage[:, :, slot, :], in_=accv[:].rearrange("p (h d) -> p h d", h=V_HEADS))
+
+            if slot == STORE_BLOCKS - 1:
+                blocks = slice(i - slot, i + 1)
+                qk_head = QK_HEADS * (r % 2)
+                nc.sync.dma_start(out=out_views[r // 2][:, qk_head : qk_head + QK_HEADS, blocks, :], in_=qk_stage[:])
+                nc.sync.dma_start(out=out_views[2][:, V_HEADS * r : V_HEADS * r + V_HEADS, blocks, :], in_=v_stage[:])
+
+        transpose_weights(0, range(ROW_BLOCKS))
+        quantise_weights(0)
+        for r in range(ROUNDS):
+            for i in range(T_BLOCKS):
+                if r == 0 and i % 2 == 0:
+                    prepare_query(i // 2)
+                if r + 1 < ROUNDS and i == FIRST_BUNCH_AT:
+                    transpose_weights(r + 1, range(0, ROW_BLOCKS // 2))
+                if r + 1 < ROUNDS and i == SECOND_BUNCH_AT:
+                    transpose_weights(r + 1, range(ROW_BLOCKS // 2, ROW_BLOCKS))
+                    quantise_weights(r + 1)
+                project_and_rotate(r, i)

@@ -20,25 +20,19 @@ HEAD = 128
 PAIRS = HEAD // 2
 K_PASS = 4 * P
 PASSES = E // K_PASS
-WORDS = E // 2
 T_BLOCKS = T // P
 ROUNDS = 4
 QK_COLS = 512
-V_COLS = 256
 QK_HEADS = QK_COLS // HEAD
-V_HEADS = V_COLS // HEAD
-ROW_BLOCKS = (QK_COLS + V_COLS) // P
-STORE_BLOCKS = 4
-FIRST_BUNCH_AT = 2
-SECOND_BUNCH_AT = 5
+W_BLOCKS = QK_COLS // P
+V_FIRST = [0, 0, 256, 512]
+V_COLS = [0, 256, 256, 512]
 
 FLOPS = 2 * T * E * 3 * E
 
 FREQ_RATIO = math.exp(-math.log(10000.0) * 2.0 / HEAD)
 TWO_PI = 2.0 * math.pi
 ROUND_MAGIC = 1.5 * 2.0**23
-TWO_PI_HIGH = 6.28125
-TWO_PI_REST = TWO_PI - TWO_PI_HIGH
 
 
 def tile_mimistreamingmultiheadattention_pa_kernel(tc, query, in_proj_w, out_0, out_1, out_2):
@@ -49,49 +43,63 @@ def tile_mimistreamingmultiheadattention_pa_kernel(tc, query, in_proj_w, out_0, 
         loads = ctx.enter_context(tc.tile_pool(name="loads", bufs=1))
         grouped_pool = ctx.enter_context(tc.tile_pool(name="grouped", bufs=2))
         mx = ctx.enter_context(tc.tile_pool(name="mx", bufs=1))
-        work = ctx.enter_context(tc.tile_pool(name="work", bufs=3))
+        work = ctx.enter_context(tc.tile_pool(name="work", bufs=4))
         stage = ctx.enter_context(tc.tile_pool(name="stage", bufs=4))
         tp_pool = ctx.enter_context(tc.psum_pool(name="tp", bufs=3))
         acc_pool = ctx.enter_context(tc.psum_pool(name="acc", bufs=3))
         accv_pool = ctx.enter_context(tc.psum_pool(name="accv", bufs=2))
+        ctx.enter_context(tc.manual_schedule())
 
         q_sb = loads.tile([P, T_BLOCKS, E], BF16)
         q_rows = query.rearrange("b (p i) k -> p (b i) k", i=T_BLOCKS)
         w_sb = {}
+        v_sb = {}
         for r in range(ROUNDS):
-            w_sb[r] = loads.tile([P, ROW_BLOCKS, E], BF16, name="w_sb%d" % r)
+            w_sb[r] = loads.tile([P, W_BLOCKS, E], BF16, name="w_sb%d" % r)
+            if V_COLS[r]:
+                v_sb[r] = loads.tile([P, V_COLS[r] // P, E], BF16, name="v_sb%d" % r)
 
-        def load_query(pair):
-            nc.sync.dma_start(out=q_sb[:, 2 * pair : 2 * pair + 2, :], in_=q_rows[:, 2 * pair : 2 * pair + 2, :])
+        def load_query(first, count):
+            nc.sync.dma_start(out=q_sb[:, first : first + count, :], in_=q_rows[:, first : first + count, :])
 
-        def load_weights(r, first_block, first_row):
-            rows = in_proj_w[first_row : first_row + 2 * P, :].rearrange("(b p) k -> p b k", p=P)
-            nc.sync.dma_start(out=w_sb[r][:, first_block : first_block + 2, :], in_=rows)
+        def load_rows(dst, first_row, count):
+            rows = in_proj_w[first_row : first_row + count * P, :].rearrange("(b p) k -> p b k", p=P)
+            nc.sync.dma_start(out=dst, in_=rows)
 
-        def load_round(r):
-            load_weights(r, 0, QK_COLS * r)
-            load_weights(r, 2, QK_COLS * r + 2 * P)
-            load_weights(r, 4, 2 * E + V_COLS * r)
+        def load_w(r, first, count):
+            load_rows(w_sb[r][:, first : first + count, :], QK_COLS * r + P * first, count)
 
-        load_weights(0, 0, 0)
-        load_weights(0, 2, 2 * P)
-        load_query(0)
-        load_weights(0, 4, 2 * E)
-        for pair in range(1, T_BLOCKS // 2):
-            load_query(pair)
-        for r in range(1, ROUNDS):
-            load_round(r)
+        def load_v(r):
+            load_rows(v_sb[r][:], 2 * E + V_FIRST[r], V_COLS[r] // P)
+
+        load_w(0, 0, 1)
+        load_query(0, 1)
+        load_w(0, 1, 1)
+        load_w(0, 2, 1)
+        load_w(0, 3, 1)
+        load_query(1, 1)
+        load_query(2, 2)
+        load_w(1, 0, 2)
+        load_query(4, 2)
+        load_w(1, 2, 2)
+        load_query(6, 2)
+        load_v(1)
+        load_w(2, 0, 2)
+        load_w(2, 2, 2)
+        load_v(2)
+        load_w(3, 0, 2)
+        load_w(3, 2, 2)
+        load_v(3)
 
         ident = const.tile([P, P], F32)
         make_identity(nc, ident[:])
-
         pos_int = const.tile([P, T_BLOCKS], I32)
         nc.gpsimd.iota(pos_int[:], pattern=[[1, T_BLOCKS]], base=0, channel_multiplier=T_BLOCKS)
-        pos = const.tile([P, T_BLOCKS], F32)
-        nc.vector.tensor_copy(out=pos[:], in_=pos_int[:])
 
         freq = const.tile([P, PAIRS], F32)
         nc.vector.memset(freq[:, 0:1], 1.0)
+        warm = const.tile([P, 1], F32)
+        nc.scalar.activation(out=warm[:], in_=freq[:, 0:1], func=ACT.Sin)
         for doubling in range(6):
             width = 2**doubling
             nc.vector.tensor_scalar(
@@ -101,185 +109,233 @@ def tile_mimistreamingmultiheadattention_pa_kernel(tc, query, in_proj_w, out_0, 
                 scalar2=None,
                 op0=ALU.mult,
             )
+        pos = const.tile([P, T_BLOCKS], F32)
+        nc.vector.tensor_copy(out=pos[:], in_=pos_int[:])
 
         table_shape = [P, T_BLOCKS, PAIRS]
-        angle = scratch.tile(table_shape, F32)
-        nc.vector.tensor_tensor(
-            out=angle[:],
-            in0=pos[:].unsqueeze(2).to_broadcast(table_shape),
-            in1=freq[:].unsqueeze(1).to_broadcast(table_shape),
-            op=ALU.mult,
-        )
 
         def flat(tile_ap):
             return tile_ap.rearrange("p i j -> p (i j)")
 
         turns = scratch.tile(table_shape, F32)
-        nc.vector.tensor_scalar(
-            out=flat(turns[:]), in0=flat(angle[:]), scalar1=1.0 / TWO_PI, scalar2=ROUND_MAGIC, op0=ALU.mult, op1=ALU.add
-        )
-        whole = scratch.tile(table_shape, F32)
-        nc.vector.tensor_scalar(
-            out=flat(whole[:]), in0=flat(turns[:]), scalar1=ROUND_MAGIC, scalar2=-TWO_PI_HIGH, op0=ALU.subtract, op1=ALU.mult
-        )
-        rest_high = scratch.tile(table_shape, F32)
-        nc.vector.tensor_tensor(out=flat(rest_high[:]), in0=flat(angle[:]), in1=flat(whole[:]), op=ALU.add)
-        rest = scratch.tile(table_shape, F32)
         nc.vector.scalar_tensor_tensor(
-            out=flat(rest[:]),
-            in0=flat(whole[:]),
-            scalar=TWO_PI_REST / TWO_PI_HIGH,
-            in1=flat(rest_high[:]),
+            out=turns[:],
+            in0=pos[:].unsqueeze(2).to_broadcast(table_shape),
+            scalar=1.0 / TWO_PI,
+            in1=freq[:].unsqueeze(1).to_broadcast(table_shape),
             op0=ALU.mult,
-            op1=ALU.add,
+            op1=ALU.mult,
         )
-
-        sin_half = scratch.tile(table_shape, F32)
-        nc.scalar.activation(out=flat(sin_half[:]), in_=flat(rest[:]), func=ACT.Sin, scale=0.5)
-        sin_quarter = scratch.tile(table_shape, F32)
-        nc.scalar.activation(out=flat(sin_quarter[:]), in_=flat(rest[:]), func=ACT.Sin, scale=0.25)
-        sq_half = scratch.tile(table_shape, F32)
-        nc.scalar.activation(out=flat(sq_half[:]), in_=flat(sin_half[:]), func=ACT.Square)
-        sq_quarter = scratch.tile(table_shape, F32)
-        nc.scalar.activation(out=flat(sq_quarter[:]), in_=flat(sin_quarter[:]), func=ACT.Square)
+        near_sin = scratch.tile(table_shape, F32)
+        nc.vector.tensor_scalar(
+            out=flat(near_sin[:]), in0=flat(turns[:]), scalar1=ROUND_MAGIC, scalar2=None, op0=ALU.add
+        )
+        near_cos = scratch.tile(table_shape, F32)
+        nc.vector.tensor_scalar(
+            out=flat(near_cos[:]), in0=flat(turns[:]), scalar1=0.25, scalar2=ROUND_MAGIC, op0=ALU.add, op1=ALU.add
+        )
+        back_sin = scratch.tile(table_shape, F32)
+        nc.vector.scalar_tensor_tensor(
+            out=flat(back_sin[:]), in0=flat(near_sin[:]), scalar=ROUND_MAGIC, in1=flat(turns[:]), op0=ALU.subtract, op1=ALU.subtract
+        )
+        back_cos = scratch.tile(table_shape, F32)
+        nc.vector.scalar_tensor_tensor(
+            out=flat(back_cos[:]), in0=flat(near_cos[:]), scalar=ROUND_MAGIC, in1=flat(turns[:]), op0=ALU.subtract, op1=ALU.subtract
+        )
 
         cos = const.tile(table_shape, F32)
-        nc.vector.tensor_scalar(
-            out=flat(cos[:]), in0=flat(sq_half[:]), scalar1=-2.0, scalar2=1.0, op0=ALU.mult, op1=ALU.add
-        )
-        twice_cos_half = scratch.tile(table_shape, F32)
-        nc.vector.tensor_scalar(
-            out=flat(twice_cos_half[:]), in0=flat(sq_quarter[:]), scalar1=-4.0, scalar2=2.0, op0=ALU.mult, op1=ALU.add
-        )
         sin_pm = const.tile([P, T_BLOCKS, 2, PAIRS], F32)
-        nc.vector.scalar_tensor_tensor(
-            out=sin_pm[:, :, 0, :], in0=sin_half[:], scalar=-1.0, in1=twice_cos_half[:], op0=ALU.mult, op1=ALU.mult
-        )
-        nc.vector.tensor_tensor(out=sin_pm[:, :, 1, :], in0=sin_half[:], in1=twice_cos_half[:], op=ALU.mult)
 
-        def transpose_block(src_words, dst_words):
+        def cos_table(blocks):
+            nc.scalar.activation(out=cos[:, blocks, :], in_=back_cos[:, blocks, :], func=ACT.Sin, scale=-TWO_PI, bias=math.pi / 2)
+
+        def sin_table(blocks):
+            nc.scalar.activation(out=sin_pm[:, blocks, 0, :], in_=back_sin[:, blocks, :], func=ACT.Sin, scale=TWO_PI)
+            nc.scalar.activation(out=sin_pm[:, blocks, 1, :], in_=back_sin[:, blocks, :], func=ACT.Sin, scale=-TWO_PI)
+
+        def transpose_block(src_words, dst_words, copy):
             tp = tp_pool.tile([P, PASSES, 2, P], F32)
             for g in range(PASSES):
                 for u in range(2):
                     first = 2 * P * g + u
                     nc.tensor.transpose(tp[:, g, u, :], src_words[:, first : 2 * P * (g + 1) : 2], ident[:])
-            nc.scalar.copy(out=dst_words, in_=tp[:].rearrange("p g u r -> p g r u"))
+            copy(out=dst_words, in_=tp[:].rearrange("p g u r -> p g r u"))
 
-        def quantise(grouped, codes, scales):
+        q_codes = mx.tile([P, T_BLOCKS, PASSES, P], U32, align_bytes=64)
+        q_scales = mx.tile([P, T_BLOCKS, PASSES, P], U8, align_bytes=64)
+        q_grouped = {}
+
+        def transpose_query(i, copy):
+            q_grouped[i] = grouped_pool.tile([P, PASSES, P, 4], BF16, tag="q_grouped", name="q_grouped%d" % i, align_bytes=64)
+            transpose_block(q_sb[:].bitcast(F32)[:, i, :], q_grouped[i][:].bitcast(F32), copy)
+
+        def quantise_query(i):
             nc.vector.quantize_mx(
-                out=codes.rearrange("p g c -> p (g c)").bitcast(FP8X4),
-                scales=scales.rearrange("p g c -> p (g c)"),
-                in_=grouped.rearrange("p g c t -> p (g c t)"),
+                out=q_codes[:, i].rearrange("p g c -> p (g c)").bitcast(FP8X4),
+                scales=q_scales[:, i].rearrange("p g c -> p (g c)"),
+                in_=q_grouped[i][:].rearrange("p g c t -> p (g c t)"),
             )
 
-        q_codes = mx.tile([P, T_BLOCKS // 2, PASSES, 2 * P], U32, align_bytes=64)
-        q_scales = mx.tile([P, T_BLOCKS // 2, PASSES, 2 * P], U8, align_bytes=64)
+        rows_sb = {}
+        grouped = {}
+        codes = {}
+        scales = {}
+        for r in range(ROUNDS):
+            for kind, source, cols in (("w", w_sb, QK_COLS), ("v", v_sb, V_COLS[r])):
+                if cols:
+                    rows_sb[kind, r] = source[r]
+                    codes[kind, r] = mx.tile([P, PASSES, cols], U32, name="%s_codes%d" % (kind, r), align_bytes=64)
+                    scales[kind, r] = mx.tile([P, PASSES, cols], U8, name="%s_scales%d" % (kind, r), align_bytes=64)
 
-        def prepare_query(pair):
-            q_grouped = grouped_pool.tile([P, PASSES, 2 * P, 4], BF16, align_bytes=64)
-            for half in range(2):
-                transpose_block(
-                    q_sb[:].bitcast(F32)[:, 2 * pair + half, :],
-                    q_grouped[:].bitcast(F32)[:, :, P * half : P * half + P, :],
+        def transpose_rows(kind, r, b, copy):
+            if b == 0:
+                cols = QK_COLS if kind == "w" else V_COLS[r]
+                grouped[kind, r] = grouped_pool.tile(
+                    [P, PASSES, cols, 4], BF16, tag="%s_grouped" % kind, name="%s_grouped%d" % (kind, r), align_bytes=64
                 )
-            quantise(q_grouped[:], q_codes[:, pair], q_scales[:, pair])
+            dst = grouped[kind, r][:].bitcast(F32)[:, :, P * b : P * b + P, :]
+            transpose_block(rows_sb[kind, r][:].bitcast(F32)[:, b, :], dst, copy)
 
-        qk_grouped = {}
-        v_grouped = {}
-        qk_codes = {}
-        qk_scales = {}
-        v_codes = {}
-        v_scales = {}
+        def quantise_rows(kind, r, g, cols):
+            nc.vector.quantize_mx(
+                out=codes[kind, r][:, g, cols].bitcast(FP8X4),
+                scales=scales[kind, r][:, g, cols],
+                in_=grouped[kind, r][:, g, cols, :].rearrange("p c t -> p (c t)"),
+            )
 
-        def transpose_weights(r, blocks):
-            if r not in qk_grouped:
-                qk_grouped[r] = grouped_pool.tile([P, PASSES, QK_COLS, 4], BF16, tag="qk_grouped", name="qk_grouped%d" % r, align_bytes=64)
-                v_grouped[r] = grouped_pool.tile([P, PASSES, V_COLS, 4], BF16, tag="v_grouped", name="v_grouped%d" % r, align_bytes=64)
-            for b in blocks:
-                if b < QK_COLS // P:
-                    dst = qk_grouped[r][:].bitcast(F32)[:, :, P * b : P * b + P, :]
-                else:
-                    first = P * b - QK_COLS
-                    dst = v_grouped[r][:].bitcast(F32)[:, :, first : first + P, :]
-                transpose_block(w_sb[r][:].bitcast(F32)[:, b, :], dst)
-
-        def quantise_weights(r):
-            qk_codes[r] = mx.tile([P, PASSES, QK_COLS], U32, name="qk_codes%d" % r, align_bytes=64)
-            qk_scales[r] = mx.tile([P, PASSES, QK_COLS], U8, name="qk_scales%d" % r, align_bytes=64)
-            v_codes[r] = mx.tile([P, PASSES, V_COLS], U32, name="v_codes%d" % r, align_bytes=64)
-            v_scales[r] = mx.tile([P, PASSES, V_COLS], U8, name="v_scales%d" % r, align_bytes=64)
-            quantise(qk_grouped[r][:], qk_codes[r][:], qk_scales[r][:])
-            quantise(v_grouped[r][:], v_codes[r][:], v_scales[r][:])
-
-        def multiply(acc, i, codes, scales):
-            cols = slice(P * (i % 2), P * (i % 2) + P)
+        def multiply(acc, i, kind, r):
             for g in range(PASSES):
                 nc.tensor.matmul_mx(
                     out=acc,
-                    lhsT=q_codes[:, i // 2, g, cols].bitcast(FP8X4),
-                    lhsT_scale=q_scales[:, i // 2, g, cols],
-                    rhs=codes[:, g, :].bitcast(FP8X4),
-                    rhs_scale=scales[:, g, :],
+                    lhsT=q_codes[:, i, g, :].bitcast(FP8X4),
+                    lhsT_scale=q_scales[:, i, g, :],
+                    rhs=codes[kind, r][:, g, :].bitcast(FP8X4),
+                    rhs_scale=scales[kind, r][:, g, :],
                     start=(g == 0),
                     stop=(g == PASSES - 1),
                 )
 
         out_views = [o.rearrange("b h (p i) d -> p (b h) i d", i=T_BLOCKS) for o in (out_0, out_1, out_2)]
+        accs = {}
         staged = {}
 
-        def project_and_rotate(r, i):
-            slot = i % STORE_BLOCKS
-            if slot == 0:
-                staged["qk"] = stage.tile([P, QK_HEADS, STORE_BLOCKS, HEAD], F32, tag="qk_stage", name="qk_stage")
-                staged["v"] = stage.tile([P, V_HEADS, STORE_BLOCKS, HEAD], F32, tag="v_stage", name="v_stage")
-            qk_stage = staged["qk"]
-            v_stage = staged["v"]
+        def multiply_qk(s):
+            accs[s] = acc_pool.tile([P, QK_COLS], F32, tag="acc", name="acc%d" % s)
+            multiply(accs[s][:], s % T_BLOCKS, "w", s // T_BLOCKS)
 
-            acc = acc_pool.tile([P, QK_COLS], F32)
-            multiply(acc[:], i, qk_codes[r], qk_scales[r])
-            accv = accv_pool.tile([P, V_COLS], F32)
-            multiply(accv[:], i, v_codes[r], v_scales[r])
+        def store_group(r, i):
+            if r < ROUNDS - 1 or i < 4:
+                return i - i % 4, 4
+            if i < 6:
+                return 4, 2
+            return i, 1
 
+        def rotate(s):
+            r, i = divmod(s, T_BLOCKS)
+            first, count = store_group(r, i)
+            if i == first:
+                staged["qk"] = stage.tile([P, QK_HEADS, count, HEAD], F32, tag="qk_stage", name="qk_stage%d" % s)
+            acc = accs[s]
             pair_shape = [P, QK_HEADS, PAIRS, 2]
+            pairs = acc[:].rearrange("p (h j e) -> p h j e", h=QK_HEADS, e=2)
             with_cos = work.tile([P, QK_COLS], F32)
             nc.vector.tensor_tensor(
                 out=with_cos[:].rearrange("p (h j e) -> p h j e", h=QK_HEADS, e=2),
-                in0=acc[:].rearrange("p (h j e) -> p h j e", h=QK_HEADS, e=2),
+                in0=pairs,
                 in1=cos[:, i, :].unsqueeze(1).unsqueeze(3).to_broadcast(pair_shape),
                 op=ALU.mult,
             )
-            with_sin = work.tile([P, 2, QK_COLS // 2], F32)
-            by_parity = acc[:].rearrange("p (h j e) -> p e h j", h=QK_HEADS, e=2)
-            for e in range(2):
-                nc.vector.tensor_tensor(
-                    out=with_sin[:, e, :].rearrange("p (h j) -> p h j", h=QK_HEADS),
-                    in0=by_parity[:, 1 - e],
-                    in1=sin_pm[:, i, e, :].unsqueeze(1).to_broadcast([P, QK_HEADS, PAIRS]),
-                    op=ALU.mult,
-                )
+            with_sin = work.tile([P, QK_COLS], F32)
+            nc.vector.tensor_tensor(
+                out=with_sin[:].rearrange("p (h j e) -> p h j e", h=QK_HEADS, e=2),
+                in0=pairs[:, :, :, ::-1],
+                in1=sin_pm[:, i].rearrange("p e j -> p j e").unsqueeze(1).to_broadcast(pair_shape),
+                op=ALU.mult,
+            )
             nc.gpsimd.tensor_tensor(
-                out=qk_stage[:, :, slot, :].rearrange("p h (j e) -> p h j e", e=2),
-                in0=with_cos[:].rearrange("p (h j e) -> p h j e", h=QK_HEADS, e=2),
-                in1=with_sin[:].rearrange("p e (h j) -> p h j e", h=QK_HEADS),
+                out=staged["qk"][:, :, i - first, :],
+                in0=with_cos[:].rearrange("p (h d) -> p h d", h=QK_HEADS),
+                in1=with_sin[:].rearrange("p (h d) -> p h d", h=QK_HEADS),
                 op=ALU.add,
             )
-            nc.scalar.copy(out=v_stage[:, :, slot, :], in_=accv[:].rearrange("p (h d) -> p h d", h=V_HEADS))
+            if i == first + count - 1:
+                head = QK_HEADS * (r % 2)
+                nc.sync.dma_start(
+                    out=out_views[r // 2][:, head : head + QK_HEADS, first : first + count, :], in_=staged["qk"][:]
+                )
 
-            if slot == STORE_BLOCKS - 1:
-                blocks = slice(i - slot, i + 1)
-                qk_head = QK_HEADS * (r % 2)
-                nc.sync.dma_start(out=out_views[r // 2][:, qk_head : qk_head + QK_HEADS, blocks, :], in_=qk_stage[:])
-                nc.sync.dma_start(out=out_views[2][:, V_HEADS * r : V_HEADS * r + V_HEADS, blocks, :], in_=v_stage[:])
+        def project_v(s):
+            r, i = divmod(s, T_BLOCKS)
+            heads = V_COLS[r] // HEAD
+            if not heads:
+                return
+            if i % 4 == 0:
+                staged["v"] = stage.tile([P, heads, 4, HEAD], F32, tag="v_stage", name="v_stage%d" % s)
+            accv = accv_pool.tile([P, V_COLS[r]], F32, tag="accv", name="accv%d" % s)
+            multiply(accv[:], i, "v", r)
+            nc.scalar.copy(out=staged["v"][:, :, i % 4, :], in_=accv[:].rearrange("p (h d) -> p h d", h=heads))
+            if i % 4 == 3:
+                head = V_FIRST[r] // HEAD
+                nc.sync.dma_start(out=out_views[2][:, head : head + heads, i - 3 : i + 1, :], in_=staged["v"][:])
 
-        transpose_weights(0, range(ROW_BLOCKS))
-        quantise_weights(0)
-        for r in range(ROUNDS):
-            for i in range(T_BLOCKS):
-                if r == 0 and i % 2 == 0:
-                    prepare_query(i // 2)
-                if r + 1 < ROUNDS and i == FIRST_BUNCH_AT:
-                    transpose_weights(r + 1, range(0, ROW_BLOCKS // 2))
-                if r + 1 < ROUNDS and i == SECOND_BUNCH_AT:
-                    transpose_weights(r + 1, range(ROW_BLOCKS // 2, ROW_BLOCKS))
-                    quantise_weights(r + 1)
-                project_and_rotate(r, i)
+        scalar_copy = nc.scalar.copy
+        vector_copy = nc.vector.tensor_copy
+
+        def quantise_first(b):
+            for g in range(PASSES):
+                quantise_rows("w", 0, g, slice(P * b, P * b + P))
+
+        transpose_rows("w", 0, 0, scalar_copy)
+        cos_table(slice(0, 2))
+        transpose_query(0, vector_copy)
+        quantise_first(0)
+        quantise_query(0)
+        transpose_rows("w", 0, 1, scalar_copy)
+        sin_table(slice(0, 2))
+        quantise_first(1)
+        transpose_rows("w", 0, 2, vector_copy)
+        transpose_rows("w", 0, 3, scalar_copy)
+        quantise_first(2)
+        quantise_first(3)
+        multiply_qk(0)
+        transpose_query(1, scalar_copy)
+        transpose_query(2, scalar_copy)
+        cos_table(slice(2, T_BLOCKS))
+        sin_table(slice(2, T_BLOCKS))
+        quantise_query(1)
+
+        prepare = {}
+        for i in range(3, T_BLOCKS):
+            prepare.setdefault(i - 3, []).append(("q", 0, i))
+        for r in range(1, ROUNDS):
+            base = T_BLOCKS * (r - 1)
+            steps_of_w = (1, 3, 4, 5) if r == 1 else (0, 1, 2, 3)
+            for b, i in enumerate(steps_of_w):
+                prepare.setdefault(base + i, []).append(("w", r, b))
+            for b in range(V_COLS[r] // P):
+                i = 4 + b if V_COLS[r] == QK_COLS else (6 if r == 1 else 4) + b
+                prepare.setdefault(base + i, []).append(("v", r, b))
+
+        def quantise_prepared(kind, r, b):
+            if kind == "q":
+                quantise_query(b)
+            elif b == (QK_COLS if kind == "w" else V_COLS[r]) // P - 1:
+                cols = QK_COLS if kind == "w" else V_COLS[r]
+                for g in range(PASSES):
+                    quantise_rows(kind, r, g, slice(0, cols))
+
+        last = T_BLOCKS * ROUNDS - 1
+        prepare[-1] = [("q", 0, 2)]
+        for s in range(last + 1):
+            before = prepare.get(s - 1, [])
+            if s < last:
+                multiply_qk(s + 1)
+            rotate(s)
+            for item in before:
+                quantise_prepared(*item)
+            for kind, r, b in prepare.get(s, []):
+                if kind == "q":
+                    transpose_query(b, scalar_copy)
+                else:
+                    transpose_rows(kind, r, b, scalar_copy)
+            project_v(s)

@@ -45,9 +45,10 @@ def tile_mimistreamingmultiheadattention_pa_kernel(tc, query, in_proj_w, out_0, 
         mx = ctx.enter_context(tc.tile_pool(name="mx", bufs=1))
         work = ctx.enter_context(tc.tile_pool(name="work", bufs=4))
         stage = ctx.enter_context(tc.tile_pool(name="stage", bufs=4))
-        tp_pool = ctx.enter_context(tc.psum_pool(name="tp", bufs=3))
+        v_stage = ctx.enter_context(tc.tile_pool(name="v_stage", bufs=3))
+        tp_pool = ctx.enter_context(tc.psum_pool(name="tp", bufs=4))
         acc_pool = ctx.enter_context(tc.psum_pool(name="acc", bufs=3))
-        accv_pool = ctx.enter_context(tc.psum_pool(name="accv", bufs=2))
+        accv_pool = ctx.enter_context(tc.psum_pool(name="accv", bufs=1))
         ctx.enter_context(tc.manual_schedule())
 
         q_sb = loads.tile([P, T_BLOCKS, E], BF16)
@@ -165,15 +166,19 @@ def tile_mimistreamingmultiheadattention_pa_kernel(tc, query, in_proj_w, out_0, 
         q_scales = mx.tile([P, T_BLOCKS, PASSES, P], U8, align_bytes=64)
         q_grouped = {}
 
-        def transpose_query(i, copy):
-            q_grouped[i] = grouped_pool.tile([P, PASSES, P, 4], BF16, tag="q_grouped", name="q_grouped%d" % i, align_bytes=64)
-            transpose_block(q_sb[:].bitcast(F32)[:, i, :], q_grouped[i][:].bitcast(F32), copy)
+        def transpose_query(first, count, copy):
+            q_grouped[first] = grouped_pool.tile(
+                [P, count, PASSES, P, 4], BF16, tag="q_grouped", name="q_grouped%d" % first, align_bytes=64
+            )
+            for n in range(count):
+                transpose_block(q_sb[:].bitcast(F32)[:, first + n, :], q_grouped[first][:].bitcast(F32)[:, n], copy)
 
-        def quantise_query(i):
+        def quantise_query(first, count):
+            blocks = slice(first, first + count)
             nc.vector.quantize_mx(
-                out=q_codes[:, i].rearrange("p g c -> p (g c)").bitcast(FP8X4),
-                scales=q_scales[:, i].rearrange("p g c -> p (g c)"),
-                in_=q_grouped[i][:].rearrange("p g c t -> p (g c t)"),
+                out=q_codes[:, blocks].rearrange("p i g c -> p (i g c)").bitcast(FP8X4),
+                scales=q_scales[:, blocks].rearrange("p i g c -> p (i g c)"),
+                in_=q_grouped[first][:].rearrange("p i g c t -> p (i g c t)"),
             )
 
         rows_sb = {}
@@ -196,7 +201,14 @@ def tile_mimistreamingmultiheadattention_pa_kernel(tc, query, in_proj_w, out_0, 
             dst = grouped[kind, r][:].bitcast(F32)[:, :, P * b : P * b + P, :]
             transpose_block(rows_sb[kind, r][:].bitcast(F32)[:, b, :], dst, copy)
 
-        def quantise_rows(kind, r, g, cols):
+        def quantise_rows(kind, r):
+            nc.vector.quantize_mx(
+                out=codes[kind, r][:].rearrange("p g c -> p (g c)").bitcast(FP8X4),
+                scales=scales[kind, r][:].rearrange("p g c -> p (g c)"),
+                in_=grouped[kind, r][:].rearrange("p g c t -> p (g c t)"),
+            )
+
+        def quantise_part(kind, r, g, cols):
             nc.vector.quantize_mx(
                 out=codes[kind, r][:, g, cols].bitcast(FP8X4),
                 scales=scales[kind, r][:, g, cols],
@@ -270,7 +282,7 @@ def tile_mimistreamingmultiheadattention_pa_kernel(tc, query, in_proj_w, out_0, 
             if not heads:
                 return
             if i % 4 == 0:
-                staged["v"] = stage.tile([P, heads, 4, HEAD], F32, tag="v_stage", name="v_stage%d" % s)
+                staged["v"] = v_stage.tile([P, heads, 4, HEAD], F32, tag="v_stage", name="v_stage%d" % s)
             accv = accv_pool.tile([P, V_COLS[r]], F32, tag="accv", name="accv%d" % s)
             multiply(accv[:], i, "v", r)
             nc.scalar.copy(out=staged["v"][:, :, i % 4, :], in_=accv[:].rearrange("p (h d) -> p h d", h=heads))
@@ -283,59 +295,67 @@ def tile_mimistreamingmultiheadattention_pa_kernel(tc, query, in_proj_w, out_0, 
 
         def quantise_first(b):
             for g in range(PASSES):
-                quantise_rows("w", 0, g, slice(P * b, P * b + P))
+                quantise_part("w", 0, g, slice(P * b, P * b + P))
 
         transpose_rows("w", 0, 0, scalar_copy)
         cos_table(slice(0, 2))
-        transpose_query(0, vector_copy)
+        transpose_query(0, 1, vector_copy)
         quantise_first(0)
-        quantise_query(0)
+        quantise_query(0, 1)
         transpose_rows("w", 0, 1, scalar_copy)
         sin_table(slice(0, 2))
         quantise_first(1)
         transpose_rows("w", 0, 2, vector_copy)
         transpose_rows("w", 0, 3, scalar_copy)
         quantise_first(2)
+        transpose_query(1, 1, scalar_copy)
         quantise_first(3)
         multiply_qk(0)
-        transpose_query(1, scalar_copy)
-        transpose_query(2, scalar_copy)
+        quantise_query(1, 1)
+        transpose_query(2, 2, scalar_copy)
         cos_table(slice(2, T_BLOCKS))
         sin_table(slice(2, T_BLOCKS))
-        quantise_query(1)
 
-        prepare = {}
-        for i in range(3, T_BLOCKS):
-            prepare.setdefault(i - 3, []).append(("q", 0, i))
-        for r in range(1, ROUNDS):
-            base = T_BLOCKS * (r - 1)
-            steps_of_w = (1, 3, 4, 5) if r == 1 else (0, 1, 2, 3)
-            for b, i in enumerate(steps_of_w):
-                prepare.setdefault(base + i, []).append(("w", r, b))
-            for b in range(V_COLS[r] // P):
-                i = 4 + b if V_COLS[r] == QK_COLS else (6 if r == 1 else 4) + b
-                prepare.setdefault(base + i, []).append(("v", r, b))
-
-        def quantise_prepared(kind, r, b):
-            if kind == "q":
-                quantise_query(b)
-            elif b == (QK_COLS if kind == "w" else V_COLS[r]) // P - 1:
-                cols = QK_COLS if kind == "w" else V_COLS[r]
-                for g in range(PASSES):
-                    quantise_rows(kind, r, g, slice(0, cols))
+        to_transpose = {
+            1: [("q", 4)],
+            2: [("w", 1, 0), ("w", 1, 1)],
+            3: [("q", 6)],
+            4: [("w", 1, 2), ("w", 1, 3)],
+            6: [("v", 1, 0), ("v", 1, 1)],
+            8: [("w", 2, 0), ("w", 2, 1)],
+            10: [("w", 2, 2), ("w", 2, 3)],
+            12: [("v", 2, 0), ("v", 2, 1)],
+            16: [("w", 3, 0), ("w", 3, 1)],
+            18: [("w", 3, 2), ("w", 3, 3)],
+            20: [("v", 3, 0), ("v", 3, 1)],
+            22: [("v", 3, 2), ("v", 3, 3)],
+        }
+        to_quantise = {
+            0: ("q", 2),
+            2: ("q", 4),
+            4: ("q", 6),
+            5: ("w", 1),
+            7: ("v", 1),
+            11: ("w", 2),
+            13: ("v", 2),
+            19: ("w", 3),
+            23: ("v", 3),
+        }
 
         last = T_BLOCKS * ROUNDS - 1
-        prepare[-1] = [("q", 0, 2)]
         for s in range(last + 1):
-            before = prepare.get(s - 1, [])
             if s < last:
                 multiply_qk(s + 1)
             rotate(s)
-            for item in before:
-                quantise_prepared(*item)
-            for kind, r, b in prepare.get(s, []):
-                if kind == "q":
-                    transpose_query(b, scalar_copy)
+            if s in to_quantise:
+                item = to_quantise[s]
+                if item[0] == "q":
+                    quantise_query(item[1], 2)
                 else:
-                    transpose_rows(kind, r, b, scalar_copy)
+                    quantise_rows(*item)
+            for item in to_transpose.get(s, []):
+                if item[0] == "q":
+                    transpose_query(item[1], 2, scalar_copy)
+                else:
+                    transpose_rows(item[0], item[1], item[2], scalar_copy)
             project_v(s)

@@ -264,7 +264,12 @@ def tile_mimistreamingmultiheadattention_pa_kernel(tc, query, in_proj_w, out_0, 
                 in1=sin_pm[:, i].rearrange("p e j -> p j e").unsqueeze(1).to_broadcast(pair_shape),
                 op=ALU.mult,
             )
-            nc.gpsimd.tensor_tensor(
+            return with_cos, with_sin
+
+        def add(s, engine, with_cos, with_sin):
+            r, i = divmod(s, T_BLOCKS)
+            first, count = store_group(r, i)
+            engine.tensor_tensor(
                 out=staged["qk"][:, :, i - first, :],
                 in0=with_cos[:].rearrange("p (h d) -> p h d", h=QK_HEADS),
                 in1=with_sin[:].rearrange("p (h d) -> p h d", h=QK_HEADS),
@@ -310,16 +315,16 @@ def tile_mimistreamingmultiheadattention_pa_kernel(tc, query, in_proj_w, out_0, 
         quantise_first(2)
         transpose_query(1, 1, scalar_copy)
         quantise_first(3)
-        multiply_qk(0)
         quantise_query(1, 1)
         transpose_query(2, 2, scalar_copy)
+        multiply_qk(0)
         cos_table(slice(2, T_BLOCKS))
         sin_table(slice(2, T_BLOCKS))
 
         to_transpose = {
-            1: [("q", 4)],
-            2: [("w", 1, 0), ("w", 1, 1)],
-            3: [("q", 6)],
+            0: [("q", 4)],
+            1: [("w", 1, 0), ("w", 1, 1)],
+            2: [("q", 6)],
             4: [("w", 1, 2), ("w", 1, 3)],
             6: [("v", 1, 0), ("v", 1, 1)],
             8: [("w", 2, 0), ("w", 2, 1)],
@@ -332,8 +337,8 @@ def tile_mimistreamingmultiheadattention_pa_kernel(tc, query, in_proj_w, out_0, 
         }
         to_quantise = {
             0: ("q", 2),
-            2: ("q", 4),
-            4: ("q", 6),
+            1: ("q", 4),
+            3: ("q", 6),
             5: ("w", 1),
             7: ("v", 1),
             11: ("w", 2),
@@ -343,19 +348,25 @@ def tile_mimistreamingmultiheadattention_pa_kernel(tc, query, in_proj_w, out_0, 
         }
 
         last = T_BLOCKS * ROUNDS - 1
+        terms = {}
         for s in range(last + 1):
+            for item in to_transpose.get(s, []):
+                if item[0] == "q":
+                    transpose_query(item[1], 2, scalar_copy)
+                else:
+                    transpose_rows(item[0], item[1], item[2], scalar_copy)
             if s < last:
                 multiply_qk(s + 1)
-            rotate(s)
+            terms[s] = rotate(s)
+            if s % 2 == 1 and s < last:
+                add(s - 1, nc.vector, *terms[s - 1])
+                add(s, nc.gpsimd, *terms[s])
+            if s == last - 1 or s == last:
+                add(s, nc.vector, *terms[s])
             if s in to_quantise:
                 item = to_quantise[s]
                 if item[0] == "q":
                     quantise_query(item[1], 2)
                 else:
                     quantise_rows(*item)
-            for item in to_transpose.get(s, []):
-                if item[0] == "q":
-                    transpose_query(item[1], 2, scalar_copy)
-                else:
-                    transpose_rows(item[0], item[1], item[2], scalar_copy)
             project_v(s)

@@ -92,6 +92,14 @@ def tile_mimistreamingmultiheadattention_pa_kernel(tc, query, in_proj_w, out_0, 
         load_w(3, 2, 2)
         load_v(3)
 
+        zeros = const.tile([P, QK_COLS], BF16)
+        nc.vector.memset(zeros[:], 0.0)
+
+        def keep_warm(count):
+            for n in range(count):
+                dummy = accv_pool.tile([P, QK_COLS], F32, tag="accv", name="dummy")
+                nc.tensor.matmul(dummy[:], lhsT=zeros[:, 0:P], rhs=zeros[:], start=True, stop=True)
+
         ident = const.tile([P, P], F32)
         make_identity(nc, ident[:])
         pos_int = const.tile([P, T_BLOCKS], I32)
@@ -281,14 +289,12 @@ def tile_mimistreamingmultiheadattention_pa_kernel(tc, query, in_proj_w, out_0, 
                     out=out_views[r // 2][:, head : head + QK_HEADS, first : first + count, :], in_=staged["qk"][:]
                 )
 
-        def project_v(s):
-            r, i = divmod(s, T_BLOCKS)
+        def project_v(r, i, pool, pool_tag):
+            s = T_BLOCKS * r + i
             heads = V_COLS[r] // HEAD
-            if not heads:
-                return
             if i % 4 == 0:
                 staged["v"] = v_stage.tile([P, heads, 4, HEAD], F32, tag="v_stage", name="v_stage%d" % s)
-            accv = accv_pool.tile([P, V_COLS[r]], F32, tag="accv", name="accv%d" % s)
+            accv = pool.tile([P, V_COLS[r]], F32, tag=pool_tag, name="accv%d" % s)
             multiply(accv[:], i, "v", r)
             nc.scalar.copy(out=staged["v"][:, :, i % 4, :], in_=accv[:].rearrange("p (h d) -> p h d", h=heads))
             if i % 4 == 3:
@@ -302,6 +308,7 @@ def tile_mimistreamingmultiheadattention_pa_kernel(tc, query, in_proj_w, out_0, 
             for g in range(PASSES):
                 quantise_part("w", 0, g, slice(P * b, P * b + P))
 
+        keep_warm(5)
         transpose_rows("w", 0, 0, scalar_copy)
         cos_table(slice(0, 2))
         transpose_query(0, 1, vector_copy)
@@ -315,9 +322,9 @@ def tile_mimistreamingmultiheadattention_pa_kernel(tc, query, in_proj_w, out_0, 
         quantise_first(2)
         transpose_query(1, 1, scalar_copy)
         quantise_first(3)
+        multiply_qk(0)
         quantise_query(1, 1)
         transpose_query(2, 2, scalar_copy)
-        multiply_qk(0)
         cos_table(slice(2, T_BLOCKS))
         sin_table(slice(2, T_BLOCKS))
 
@@ -350,13 +357,15 @@ def tile_mimistreamingmultiheadattention_pa_kernel(tc, query, in_proj_w, out_0, 
         last = T_BLOCKS * ROUNDS - 1
         terms = {}
         for s in range(last + 1):
+            if s < last:
+                multiply_qk(s + 1)
+            if s < T_BLOCKS:
+                keep_warm(1)
             for item in to_transpose.get(s, []):
                 if item[0] == "q":
                     transpose_query(item[1], 2, scalar_copy)
                 else:
                     transpose_rows(item[0], item[1], item[2], scalar_copy)
-            if s < last:
-                multiply_qk(s + 1)
             terms[s] = rotate(s)
             if s % 2 == 1 and s < last:
                 add(s - 1, nc.vector, *terms[s - 1])
@@ -369,4 +378,10 @@ def tile_mimistreamingmultiheadattention_pa_kernel(tc, query, in_proj_w, out_0, 
                     quantise_query(item[1], 2)
                 else:
                     quantise_rows(*item)
-            project_v(s)
+            r, i = divmod(s, T_BLOCKS)
+            if r == ROUNDS - 1:
+                for v_block in (2 * i, 2 * i + 1):
+                    if v_block < T_BLOCKS:
+                        project_v(r, v_block, tp_pool, "tp")
+            elif V_COLS[r]:
+                project_v(r, i, accv_pool, "accv")

@@ -92,14 +92,6 @@ def tile_mimistreamingmultiheadattention_pa_kernel(tc, query, in_proj_w, out_0, 
         load_w(3, 2, 2)
         load_v(3)
 
-        zeros = const.tile([P, QK_COLS], BF16)
-        nc.vector.memset(zeros[:], 0.0)
-
-        def keep_warm(count):
-            for n in range(count):
-                dummy = accv_pool.tile([P, QK_COLS], F32, tag="accv", name="dummy")
-                nc.tensor.matmul(dummy[:], lhsT=zeros[:, 0:P], rhs=zeros[:], start=True, stop=True)
-
         ident = const.tile([P, P], F32)
         make_identity(nc, ident[:])
         pos_int = const.tile([P, T_BLOCKS], I32)
@@ -108,7 +100,8 @@ def tile_mimistreamingmultiheadattention_pa_kernel(tc, query, in_proj_w, out_0, 
         freq = const.tile([P, PAIRS], F32)
         nc.vector.memset(freq[:, 0:1], 1.0)
         warm = const.tile([P, 1], F32)
-        nc.scalar.activation(out=warm[:], in_=freq[:, 0:1], func=ACT.Sin)
+        nc.vector.memset(warm[:], 0.0)
+        nc.scalar.activation(out=warm[:], in_=warm[:], func=ACT.Sin)
         for doubling in range(6):
             width = 2**doubling
             nc.vector.tensor_scalar(
@@ -272,13 +265,13 @@ def tile_mimistreamingmultiheadattention_pa_kernel(tc, query, in_proj_w, out_0, 
                 in1=sin_pm[:, i].rearrange("p e j -> p j e").unsqueeze(1).to_broadcast(pair_shape),
                 op=ALU.mult,
             )
-            return with_cos, with_sin
+            return staged["qk"], with_cos, with_sin
 
-        def add(s, engine, with_cos, with_sin):
+        def add(s, engine, sums, with_cos, with_sin):
             r, i = divmod(s, T_BLOCKS)
             first, count = store_group(r, i)
             engine.tensor_tensor(
-                out=staged["qk"][:, :, i - first, :],
+                out=sums[:, :, i - first, :],
                 in0=with_cos[:].rearrange("p (h d) -> p h d", h=QK_HEADS),
                 in1=with_sin[:].rearrange("p (h d) -> p h d", h=QK_HEADS),
                 op=ALU.add,
@@ -286,7 +279,7 @@ def tile_mimistreamingmultiheadattention_pa_kernel(tc, query, in_proj_w, out_0, 
             if i == first + count - 1:
                 head = QK_HEADS * (r % 2)
                 nc.sync.dma_start(
-                    out=out_views[r // 2][:, head : head + QK_HEADS, first : first + count, :], in_=staged["qk"][:]
+                    out=out_views[r // 2][:, head : head + QK_HEADS, first : first + count, :], in_=sums[:]
                 )
 
         def project_v(r, i, pool, pool_tag):
@@ -308,7 +301,6 @@ def tile_mimistreamingmultiheadattention_pa_kernel(tc, query, in_proj_w, out_0, 
             for g in range(PASSES):
                 quantise_part("w", 0, g, slice(P * b, P * b + P))
 
-        keep_warm(5)
         transpose_rows("w", 0, 0, scalar_copy)
         cos_table(slice(0, 2))
         transpose_query(0, 1, vector_copy)
@@ -322,16 +314,18 @@ def tile_mimistreamingmultiheadattention_pa_kernel(tc, query, in_proj_w, out_0, 
         quantise_first(2)
         transpose_query(1, 1, scalar_copy)
         quantise_first(3)
-        multiply_qk(0)
+        transpose_query(2, 1, scalar_copy)
         quantise_query(1, 1)
-        transpose_query(2, 2, scalar_copy)
+        multiply_qk(0)
+        quantise_query(2, 1)
         cos_table(slice(2, T_BLOCKS))
         sin_table(slice(2, T_BLOCKS))
 
         to_transpose = {
-            0: [("q", 4)],
-            1: [("w", 1, 0), ("w", 1, 1)],
-            2: [("q", 6)],
+            0: [("q", 3, 2)],
+            1: [("q", 5, 2)],
+            2: [("w", 1, 0), ("w", 1, 1)],
+            3: [("q", 7, 1)],
             4: [("w", 1, 2), ("w", 1, 3)],
             6: [("v", 1, 0), ("v", 1, 1)],
             8: [("w", 2, 0), ("w", 2, 1)],
@@ -340,17 +334,17 @@ def tile_mimistreamingmultiheadattention_pa_kernel(tc, query, in_proj_w, out_0, 
             16: [("w", 3, 0), ("w", 3, 1)],
             18: [("w", 3, 2), ("w", 3, 3)],
             20: [("v", 3, 0), ("v", 3, 1)],
-            22: [("v", 3, 2), ("v", 3, 3)],
+            21: [("v", 3, 2), ("v", 3, 3)],
         }
         to_quantise = {
-            0: ("q", 2),
-            1: ("q", 4),
-            3: ("q", 6),
+            1: ("q", 3, 2),
+            3: ("q", 5, 2),
+            4: ("q", 7, 1),
             5: ("w", 1),
-            7: ("v", 1),
+            8: ("v", 1),
             11: ("w", 2),
-            13: ("v", 2),
-            19: ("w", 3),
+            14: ("v", 2),
+            20: ("w", 3),
             23: ("v", 3),
         }
 
@@ -359,15 +353,15 @@ def tile_mimistreamingmultiheadattention_pa_kernel(tc, query, in_proj_w, out_0, 
         for s in range(last + 1):
             if s < last:
                 multiply_qk(s + 1)
-            if s < T_BLOCKS:
-                keep_warm(1)
             for item in to_transpose.get(s, []):
                 if item[0] == "q":
-                    transpose_query(item[1], 2, scalar_copy)
+                    transpose_query(item[1], item[2], scalar_copy)
                 else:
                     transpose_rows(item[0], item[1], item[2], scalar_copy)
             terms[s] = rotate(s)
-            if s % 2 == 1 and s < last:
+            if s % 3 == 0 and s < last - 1:
+                add(s, nc.gpsimd, *terms[s])
+            if s % 3 == 2 and s < last:
                 add(s - 1, nc.vector, *terms[s - 1])
                 add(s, nc.gpsimd, *terms[s])
             if s == last - 1 or s == last:
@@ -375,7 +369,7 @@ def tile_mimistreamingmultiheadattention_pa_kernel(tc, query, in_proj_w, out_0, 
             if s in to_quantise:
                 item = to_quantise[s]
                 if item[0] == "q":
-                    quantise_query(item[1], 2)
+                    quantise_query(item[1], item[2])
                 else:
                     quantise_rows(*item)
             r, i = divmod(s, T_BLOCKS)

@@ -25,8 +25,8 @@ ROUNDS = 4
 QK_COLS = 512
 QK_HEADS = QK_COLS // HEAD
 W_BLOCKS = QK_COLS // P
-V_FIRST = [0, 0, 256, 512]
-V_COLS = [0, 256, 256, 512]
+V_FIRST = [0, 0, 256, 768]
+V_COLS = [0, 256, 512, 256]
 
 FLOPS = 2 * T * E * 3 * E
 
@@ -43,6 +43,7 @@ def tile_mimistreamingmultiheadattention_pa_kernel(tc, query, in_proj_w, out_0, 
         loads = ctx.enter_context(tc.tile_pool(name="loads", bufs=1))
         grouped_pool = ctx.enter_context(tc.tile_pool(name="grouped", bufs=2))
         mx = ctx.enter_context(tc.tile_pool(name="mx", bufs=1))
+        order_pool = ctx.enter_context(tc.tile_pool(name="order", bufs=3))
         work = ctx.enter_context(tc.tile_pool(name="work", bufs=4))
         stage = ctx.enter_context(tc.tile_pool(name="stage", bufs=4))
         v_stage = ctx.enter_context(tc.tile_pool(name="v_stage", bufs=3))
@@ -80,10 +81,9 @@ def tile_mimistreamingmultiheadattention_pa_kernel(tc, query, in_proj_w, out_0, 
         load_w(0, 3, 1)
         load_query(1, 1)
         load_query(2, 2)
+        load_query(4, 4)
         load_w(1, 0, 2)
-        load_query(4, 2)
         load_w(1, 2, 2)
-        load_query(6, 2)
         load_v(1)
         load_w(2, 0, 2)
         load_w(2, 2, 2)
@@ -136,11 +136,11 @@ def tile_mimistreamingmultiheadattention_pa_kernel(tc, query, in_proj_w, out_0, 
         nc.vector.tensor_scalar(
             out=flat(near_cos[:]), in0=flat(turns[:]), scalar1=0.25, scalar2=ROUND_MAGIC, op0=ALU.add, op1=ALU.add
         )
-        back_sin = scratch.tile(table_shape, F32)
+        back_sin = near_sin
         nc.vector.scalar_tensor_tensor(
             out=flat(back_sin[:]), in0=flat(near_sin[:]), scalar=ROUND_MAGIC, in1=flat(turns[:]), op0=ALU.subtract, op1=ALU.subtract
         )
-        back_cos = scratch.tile(table_shape, F32)
+        back_cos = near_cos
         nc.vector.scalar_tensor_tensor(
             out=flat(back_cos[:]), in0=flat(near_cos[:]), scalar=ROUND_MAGIC, in1=flat(turns[:]), op0=ALU.subtract, op1=ALU.subtract
         )
@@ -159,9 +159,17 @@ def tile_mimistreamingmultiheadattention_pa_kernel(tc, query, in_proj_w, out_0, 
             tp = tp_pool.tile([P, PASSES, 2, P], F32)
             for g in range(PASSES):
                 for u in range(2):
-                    first = 2 * P * g + u
-                    nc.tensor.transpose(tp[:, g, u, :], src_words[:, first : 2 * P * (g + 1) : 2], ident[:])
+                    nc.tensor.transpose(tp[:, g, u, :], src_words[:, g, u, :], ident[:])
             copy(out=dst_words, in_=tp[:].rearrange("p g u r -> p g r u"))
+
+        def split_words(rows):
+            return rows.bitcast(F32).rearrange("p (g w u) -> p g u w", g=PASSES, u=2)
+
+        ordered = {}
+
+        def order_words(kind, r, b):
+            ordered[kind, r, b] = order_pool.tile([P, PASSES, 2, P], F32, tag="ordered", name="ordered_%s%d%d" % (kind, r, b))
+            nc.scalar.copy(out=ordered[kind, r, b][:], in_=split_words(rows_sb[kind, r][:, b, :]))
 
         q_codes = mx.tile([P, T_BLOCKS, PASSES, P], U32, align_bytes=64)
         q_scales = mx.tile([P, T_BLOCKS, PASSES, P], U8, align_bytes=64)
@@ -172,7 +180,7 @@ def tile_mimistreamingmultiheadattention_pa_kernel(tc, query, in_proj_w, out_0, 
                 [P, count, PASSES, P, 4], BF16, tag="q_grouped", name="q_grouped%d" % first, align_bytes=64
             )
             for n in range(count):
-                transpose_block(q_sb[:].bitcast(F32)[:, first + n, :], q_grouped[first][:].bitcast(F32)[:, n], copy)
+                transpose_block(split_words(q_sb[:, first + n, :]), q_grouped[first][:].bitcast(F32)[:, n], copy)
 
         def quantise_query(first, count):
             blocks = slice(first, first + count)
@@ -197,10 +205,18 @@ def tile_mimistreamingmultiheadattention_pa_kernel(tc, query, in_proj_w, out_0, 
             if b == 0:
                 cols = QK_COLS if kind == "w" else V_COLS[r]
                 grouped[kind, r] = grouped_pool.tile(
-                    [P, PASSES, cols, 4], BF16, tag="%s_grouped" % kind, name="%s_grouped%d" % (kind, r), align_bytes=64
+                    [P, PASSES, cols, 4],
+                    BF16,
+                    tag="%s_grouped" % kind,
+                    name="%s_grouped%d" % (kind, r),
+                    bufs=2 if kind == "w" else 1,
+                    align_bytes=64,
                 )
             dst = grouped[kind, r][:].bitcast(F32)[:, :, P * b : P * b + P, :]
-            transpose_block(rows_sb[kind, r][:].bitcast(F32)[:, b, :], dst, copy)
+            if (kind, r, b) in ordered:
+                transpose_block(ordered[kind, r, b][:], dst, copy)
+            else:
+                transpose_block(split_words(rows_sb[kind, r][:, b, :]), dst, copy)
 
         def quantise_rows(kind, r):
             nc.vector.quantize_mx(
@@ -282,17 +298,23 @@ def tile_mimistreamingmultiheadattention_pa_kernel(tc, query, in_proj_w, out_0, 
                     out=out_views[r // 2][:, head : head + QK_HEADS, first : first + count, :], in_=sums[:]
                 )
 
+        def v_store_group(r, i):
+            if r < ROUNDS - 1 or i < 4:
+                return i - i % 4, 4
+            return i - i % 2, 2
+
         def project_v(r, i, pool, pool_tag):
             s = T_BLOCKS * r + i
             heads = V_COLS[r] // HEAD
-            if i % 4 == 0:
-                staged["v"] = v_stage.tile([P, heads, 4, HEAD], F32, tag="v_stage", name="v_stage%d" % s)
+            first, count = v_store_group(r, i)
+            if i == first:
+                staged["v"] = v_stage.tile([P, heads, count, HEAD], F32, tag="v_stage", name="v_stage%d" % s)
             accv = pool.tile([P, V_COLS[r]], F32, tag=pool_tag, name="accv%d" % s)
             multiply(accv[:], i, "v", r)
-            nc.scalar.copy(out=staged["v"][:, :, i % 4, :], in_=accv[:].rearrange("p (h d) -> p h d", h=heads))
-            if i % 4 == 3:
+            nc.scalar.copy(out=staged["v"][:, :, i - first, :], in_=accv[:].rearrange("p (h d) -> p h d", h=heads))
+            if i == first + count - 1:
                 head = V_FIRST[r] // HEAD
-                nc.sync.dma_start(out=out_views[2][:, head : head + heads, i - 3 : i + 1, :], in_=staged["v"][:])
+                nc.sync.dma_start(out=out_views[2][:, head : head + heads, first : i + 1, :], in_=staged["v"][:])
 
         scalar_copy = nc.scalar.copy
         vector_copy = nc.vector.tensor_copy
@@ -303,13 +325,13 @@ def tile_mimistreamingmultiheadattention_pa_kernel(tc, query, in_proj_w, out_0, 
 
         transpose_rows("w", 0, 0, scalar_copy)
         cos_table(slice(0, 2))
-        transpose_query(0, 1, vector_copy)
+        transpose_query(0, 1, scalar_copy)
         quantise_first(0)
         quantise_query(0, 1)
         transpose_rows("w", 0, 1, scalar_copy)
         sin_table(slice(0, 2))
         quantise_first(1)
-        transpose_rows("w", 0, 2, vector_copy)
+        transpose_rows("w", 0, 2, scalar_copy)
         transpose_rows("w", 0, 3, scalar_copy)
         quantise_first(2)
         transpose_query(1, 1, scalar_copy)
@@ -325,32 +347,33 @@ def tile_mimistreamingmultiheadattention_pa_kernel(tc, query, in_proj_w, out_0, 
             0: [("q", 3, 2)],
             1: [("q", 5, 2)],
             2: [("w", 1, 0), ("w", 1, 1)],
-            3: [("q", 7, 1)],
-            4: [("w", 1, 2), ("w", 1, 3)],
-            6: [("v", 1, 0), ("v", 1, 1)],
-            8: [("w", 2, 0), ("w", 2, 1)],
-            10: [("w", 2, 2), ("w", 2, 3)],
-            12: [("v", 2, 0), ("v", 2, 1)],
-            16: [("w", 3, 0), ("w", 3, 1)],
-            18: [("w", 3, 2), ("w", 3, 3)],
+            3: [("q", 7, 1), ("w", 1, 2), ("w", 1, 3)],
+            5: [("v", 1, 0), ("v", 1, 1)],
+            7: [("w", 2, 0), ("w", 2, 1)],
+            9: [("w", 2, 2), ("w", 2, 3)],
+            11: [("v", 2, 0), ("v", 2, 1)],
+            12: [("v", 2, 2), ("v", 2, 3)],
+            15: [("w", 3, 0), ("w", 3, 1)],
+            17: [("w", 3, 2), ("w", 3, 3)],
             20: [("v", 3, 0), ("v", 3, 1)],
-            21: [("v", 3, 2), ("v", 3, 3)],
         }
         to_quantise = {
-            1: ("q", 3, 2),
-            3: ("q", 5, 2),
-            4: ("q", 7, 1),
-            5: ("w", 1),
-            8: ("v", 1),
-            11: ("w", 2),
-            14: ("v", 2),
-            20: ("w", 3),
-            23: ("v", 3),
+            1: [("q", 3, 2)],
+            3: [("q", 5, 2)],
+            5: [("q", 7, 1), ("w", 1)],
+            8: [("v", 1)],
+            11: [("w", 2)],
+            14: [("v", 2)],
+            20: [("w", 3)],
+            23: [("v", 3)],
         }
 
         last = T_BLOCKS * ROUNDS - 1
         terms = {}
         for s in range(last + 1):
+            for item in to_transpose.get(s + 1, []):
+                if item[0] != "q" and item[1] >= 2:
+                    order_words(*item)
             if s < last:
                 multiply_qk(s + 1)
             for item in to_transpose.get(s, []):
@@ -359,23 +382,18 @@ def tile_mimistreamingmultiheadattention_pa_kernel(tc, query, in_proj_w, out_0, 
                 else:
                     transpose_rows(item[0], item[1], item[2], scalar_copy)
             terms[s] = rotate(s)
-            if s % 3 == 0 and s < last - 1:
+            if s in (6, 9, 12, 15, 18, 21, 24, 27,) :
                 add(s, nc.gpsimd, *terms[s])
-            if s % 3 == 2 and s < last:
+            if s in (1, 3, 5, 8, 11, 14, 17, 20, 23, 26, 29,):
+                for item in to_quantise.get(s, []):
+                    if item[0] == "q":
+                        quantise_query(item[1], item[2])
+                    else:
+                        quantise_rows(*item)
                 add(s - 1, nc.vector, *terms[s - 1])
                 add(s, nc.gpsimd, *terms[s])
             if s == last - 1 or s == last:
                 add(s, nc.vector, *terms[s])
-            if s in to_quantise:
-                item = to_quantise[s]
-                if item[0] == "q":
-                    quantise_query(item[1], item[2])
-                else:
-                    quantise_rows(*item)
             r, i = divmod(s, T_BLOCKS)
-            if r == ROUNDS - 1:
-                for v_block in (2 * i, 2 * i + 1):
-                    if v_block < T_BLOCKS:
-                        project_v(r, v_block, tp_pool, "tp")
-            elif V_COLS[r]:
-                project_v(r, i, accv_pool, "accv")
+            for v_block in ((2 * i, 2 * i + 1) if r == ROUNDS - 1 else (i,)) if r and i * (r // 3) < 4 else ():
+                project_v(r, v_block, *((tp_pool, "tp") if r >= 2 else (accv_pool, "accv")))

@@ -43,7 +43,7 @@ def tile_mimistreamingmultiheadattention_pa_kernel(tc, query, in_proj_w, out_0, 
         loads = ctx.enter_context(tc.tile_pool(name="loads", bufs=1))
         grouped_pool = ctx.enter_context(tc.tile_pool(name="grouped", bufs=2))
         mx = ctx.enter_context(tc.tile_pool(name="mx", bufs=1))
-        order_pool = ctx.enter_context(tc.tile_pool(name="order", bufs=3))
+        order_pool = ctx.enter_context(tc.tile_pool(name="order", bufs=4))
         work = ctx.enter_context(tc.tile_pool(name="work", bufs=4))
         stage = ctx.enter_context(tc.tile_pool(name="stage", bufs=4))
         v_stage = ctx.enter_context(tc.tile_pool(name="v_stage", bufs=3))
@@ -97,16 +97,17 @@ def tile_mimistreamingmultiheadattention_pa_kernel(tc, query, in_proj_w, out_0, 
         pos_int = const.tile([P, T_BLOCKS], I32)
         nc.gpsimd.iota(pos_int[:], pattern=[[1, T_BLOCKS]], base=0, channel_multiplier=T_BLOCKS)
 
-        freq = const.tile([P, PAIRS], F32)
-        nc.vector.memset(freq[:, 0:1], 1.0)
+        signed_freq = const.tile([P, PAIRS, 2], F32)
+        nc.vector.memset(signed_freq[:, 0:1, 0:1], -1.0)
+        nc.vector.memset(signed_freq[:, 0:1, 1:2], 1.0)
         warm = const.tile([P, 1], F32)
         nc.vector.memset(warm[:], 0.0)
         nc.scalar.activation(out=warm[:], in_=warm[:], func=ACT.Sin)
         for doubling in range(6):
             width = 2**doubling
             nc.vector.tensor_scalar(
-                out=freq[:, width : 2 * width],
-                in0=freq[:, 0:width],
+                out=signed_freq[:, width : 2 * width, :],
+                in0=signed_freq[:, 0:width, :],
                 scalar1=FREQ_RATIO**width,
                 scalar2=None,
                 op0=ALU.mult,
@@ -114,46 +115,50 @@ def tile_mimistreamingmultiheadattention_pa_kernel(tc, query, in_proj_w, out_0, 
         pos = const.tile([P, T_BLOCKS], F32)
         nc.vector.tensor_copy(out=pos[:], in_=pos_int[:])
 
-        table_shape = [P, T_BLOCKS, PAIRS]
-
         def flat(tile_ap):
             return tile_ap.rearrange("p i j -> p (i j)")
 
-        turns = scratch.tile(table_shape, F32)
+        signed_shape = [P, T_BLOCKS, HEAD]
+        turns = scratch.tile(signed_shape, F32)
         nc.vector.scalar_tensor_tensor(
             out=turns[:],
-            in0=pos[:].unsqueeze(2).to_broadcast(table_shape),
+            in0=pos[:].unsqueeze(2).to_broadcast(signed_shape),
             scalar=1.0 / TWO_PI,
-            in1=freq[:].unsqueeze(1).to_broadcast(table_shape),
+            in1=signed_freq[:].rearrange("p j e -> p (j e)").unsqueeze(1).to_broadcast(signed_shape),
             op0=ALU.mult,
             op1=ALU.mult,
         )
-        near_sin = scratch.tile(table_shape, F32)
+        back_sin = scratch.tile(signed_shape, F32)
         nc.vector.tensor_scalar(
-            out=flat(near_sin[:]), in0=flat(turns[:]), scalar1=ROUND_MAGIC, scalar2=None, op0=ALU.add
+            out=flat(back_sin[:]), in0=flat(turns[:]), scalar1=ROUND_MAGIC, scalar2=None, op0=ALU.add
         )
-        near_cos = scratch.tile(table_shape, F32)
+        quarter_on = turns[:].rearrange("p i (j e) -> p i j e", e=2)[:, :, :, 1]
+        back_cos = scratch.tile([P, T_BLOCKS, PAIRS], F32)
         nc.vector.tensor_scalar(
-            out=flat(near_cos[:]), in0=flat(turns[:]), scalar1=0.25, scalar2=ROUND_MAGIC, op0=ALU.add, op1=ALU.add
+            out=back_cos[:], in0=quarter_on, scalar1=0.25, scalar2=ROUND_MAGIC, op0=ALU.add, op1=ALU.add
         )
-        back_sin = near_sin
         nc.vector.scalar_tensor_tensor(
-            out=flat(back_sin[:]), in0=flat(near_sin[:]), scalar=ROUND_MAGIC, in1=flat(turns[:]), op0=ALU.subtract, op1=ALU.subtract
+            out=flat(back_sin[:]), in0=flat(back_sin[:]), scalar=ROUND_MAGIC, in1=flat(turns[:]), op0=ALU.subtract, op1=ALU.subtract
         )
-        back_cos = near_cos
         nc.vector.scalar_tensor_tensor(
-            out=flat(back_cos[:]), in0=flat(near_cos[:]), scalar=ROUND_MAGIC, in1=flat(turns[:]), op0=ALU.subtract, op1=ALU.subtract
+            out=back_cos[:], in0=back_cos[:], scalar=ROUND_MAGIC, in1=quarter_on, op0=ALU.subtract, op1=ALU.subtract
         )
 
-        cos = const.tile(table_shape, F32)
-        sin_pm = const.tile([P, T_BLOCKS, 2, PAIRS], F32)
+        cos = const.tile(signed_shape, F32)
+        sin = const.tile(signed_shape, F32)
 
         def cos_table(blocks):
-            nc.scalar.activation(out=cos[:, blocks, :], in_=back_cos[:, blocks, :], func=ACT.Sin, scale=-TWO_PI, bias=math.pi / 2)
+            count = blocks.stop - blocks.start
+            nc.scalar.activation(
+                out=cos[:, blocks, :].rearrange("p i (j e) -> p i j e", e=2),
+                in_=back_cos[:, blocks, :].unsqueeze(3).to_broadcast([P, count, PAIRS, 2]),
+                func=ACT.Sin,
+                scale=-TWO_PI,
+                bias=math.pi / 2,
+            )
 
         def sin_table(blocks):
-            nc.scalar.activation(out=sin_pm[:, blocks, 0, :], in_=back_sin[:, blocks, :], func=ACT.Sin, scale=TWO_PI)
-            nc.scalar.activation(out=sin_pm[:, blocks, 1, :], in_=back_sin[:, blocks, :], func=ACT.Sin, scale=-TWO_PI)
+            nc.scalar.activation(out=sin[:, blocks, :], in_=back_sin[:, blocks, :], func=ACT.Sin, scale=-TWO_PI)
 
         def transpose_block(src_words, dst_words, copy):
             tp = tp_pool.tile([P, PASSES, 2, P], F32)
@@ -167,9 +172,13 @@ def tile_mimistreamingmultiheadattention_pa_kernel(tc, query, in_proj_w, out_0, 
 
         ordered = {}
 
-        def order_words(kind, r, b):
+        def order_words(kind, r, b, copy=nc.scalar.copy):
+            if kind == "q":
+                rows = q_sb[:, b, :]
+            else:
+                rows = rows_sb[kind, r][:, b, :]
             ordered[kind, r, b] = order_pool.tile([P, PASSES, 2, P], F32, tag="ordered", name="ordered_%s%d%d" % (kind, r, b))
-            nc.scalar.copy(out=ordered[kind, r, b][:], in_=split_words(rows_sb[kind, r][:, b, :]))
+            copy(out=ordered[kind, r, b][:], in_=split_words(rows))
 
         q_codes = mx.tile([P, T_BLOCKS, PASSES, P], U32, align_bytes=64)
         q_scales = mx.tile([P, T_BLOCKS, PASSES, P], U8, align_bytes=64)
@@ -180,7 +189,12 @@ def tile_mimistreamingmultiheadattention_pa_kernel(tc, query, in_proj_w, out_0, 
                 [P, count, PASSES, P, 4], BF16, tag="q_grouped", name="q_grouped%d" % first, align_bytes=64
             )
             for n in range(count):
-                transpose_block(split_words(q_sb[:, first + n, :]), q_grouped[first][:].bitcast(F32)[:, n], copy)
+                i = first + n
+                if ("q", 0, i) in ordered:
+                    words = ordered["q", 0, i][:]
+                else:
+                    words = split_words(q_sb[:, i, :])
+                transpose_block(words, q_grouped[first][:].bitcast(F32)[:, n], copy)
 
         def quantise_query(first, count):
             blocks = slice(first, first + count)
@@ -232,14 +246,14 @@ def tile_mimistreamingmultiheadattention_pa_kernel(tc, query, in_proj_w, out_0, 
                 in_=grouped[kind, r][:, g, cols, :].rearrange("p c t -> p (c t)"),
             )
 
-        def multiply(acc, i, kind, r):
+        def multiply(acc, i, kind, r, cols):
             for g in range(PASSES):
                 nc.tensor.matmul_mx(
                     out=acc,
                     lhsT=q_codes[:, i, g, :].bitcast(FP8X4),
                     lhsT_scale=q_scales[:, i, g, :],
-                    rhs=codes[kind, r][:, g, :].bitcast(FP8X4),
-                    rhs_scale=scales[kind, r][:, g, :],
+                    rhs=codes[kind, r][:, g, cols].bitcast(FP8X4),
+                    rhs_scale=scales[kind, r][:, g, cols],
                     start=(g == 0),
                     stop=(g == PASSES - 1),
                 )
@@ -248,9 +262,11 @@ def tile_mimistreamingmultiheadattention_pa_kernel(tc, query, in_proj_w, out_0, 
         accs = {}
         staged = {}
 
-        def multiply_qk(s):
-            accs[s] = acc_pool.tile([P, QK_COLS], F32, tag="acc", name="acc%d" % s)
-            multiply(accs[s][:], s % T_BLOCKS, "w", s // T_BLOCKS)
+        def multiply_qk(s, first_head=0, heads=QK_HEADS):
+            acc = acc_pool.tile([P, heads * HEAD], F32, tag="acc", name="acc%d_%d" % (s, first_head))
+            cols = slice(first_head * HEAD, (first_head + heads) * HEAD)
+            multiply(acc[:], s % T_BLOCKS, "w", s // T_BLOCKS, cols)
+            accs.setdefault(s, []).append((acc, first_head, heads))
 
         def store_group(r, i):
             if r < ROUNDS - 1 or i < 4:
@@ -259,44 +275,54 @@ def tile_mimistreamingmultiheadattention_pa_kernel(tc, query, in_proj_w, out_0, 
                 return 4, 2
             return i, 1
 
+        terms = {}
+
         def rotate(s):
             r, i = divmod(s, T_BLOCKS)
             first, count = store_group(r, i)
-            if i == first:
+            if i == first and s not in terms:
                 staged["qk"] = stage.tile([P, QK_HEADS, count, HEAD], F32, tag="qk_stage", name="qk_stage%d" % s)
-            acc = accs[s]
-            pair_shape = [P, QK_HEADS, PAIRS, 2]
-            pairs = acc[:].rearrange("p (h j e) -> p h j e", h=QK_HEADS, e=2)
-            with_cos = work.tile([P, QK_COLS], F32)
-            nc.vector.tensor_tensor(
-                out=with_cos[:].rearrange("p (h j e) -> p h j e", h=QK_HEADS, e=2),
-                in0=pairs,
-                in1=cos[:, i, :].unsqueeze(1).unsqueeze(3).to_broadcast(pair_shape),
-                op=ALU.mult,
-            )
-            with_sin = work.tile([P, QK_COLS], F32)
-            nc.vector.tensor_tensor(
-                out=with_sin[:].rearrange("p (h j e) -> p h j e", h=QK_HEADS, e=2),
-                in0=pairs[:, :, :, ::-1],
-                in1=sin_pm[:, i].rearrange("p e j -> p j e").unsqueeze(1).to_broadcast(pair_shape),
-                op=ALU.mult,
-            )
-            return staged["qk"], with_cos, with_sin
+            if s not in terms:
+                with_cos = work.tile([P, QK_HEADS, PAIRS, 2], F32, tag="with_cos", name="with_cos%d" % s)
+                with_sin = work.tile([P, QK_HEADS, PAIRS, 2], F32, tag="with_sin", name="with_sin%d" % s)
+                terms[s] = (staged["qk"], with_cos, with_sin)
+            sums, with_cos, with_sin = terms[s]
+            for acc, first_head, heads in accs.pop(s):
+                part = slice(first_head, first_head + heads)
+                shape = [P, heads, PAIRS, 2]
+                pairs = acc[:].rearrange("p (h j e) -> p h j e", h=heads, e=2)
+                nc.vector.tensor_tensor(
+                    out=with_cos[:, part],
+                    in0=pairs,
+                    in1=cos[:, i, :].rearrange("p (j e) -> p j e", e=2).unsqueeze(1).to_broadcast(shape),
+                    op=ALU.mult,
+                )
+                nc.vector.tensor_tensor(
+                    out=with_sin[:, part],
+                    in0=pairs[:, :, :, ::-1],
+                    in1=sin[:, i, :].rearrange("p (j e) -> p j e", e=2).unsqueeze(1).to_broadcast(shape),
+                    op=ALU.mult,
+                )
 
-        def add(s, engine, sums, with_cos, with_sin):
+        def add(s, engine):
+            sums, with_cos, with_sin = terms[s]
             r, i = divmod(s, T_BLOCKS)
             first, count = store_group(r, i)
-            engine.tensor_tensor(
-                out=sums[:, :, i - first, :],
-                in0=with_cos[:].rearrange("p (h d) -> p h d", h=QK_HEADS),
-                in1=with_sin[:].rearrange("p (h d) -> p h d", h=QK_HEADS),
-                op=ALU.add,
-            )
-            if i == first + count - 1:
-                head = QK_HEADS * (r % 2)
-                nc.sync.dma_start(
-                    out=out_views[r // 2][:, head : head + QK_HEADS, first : first + count, :], in_=sums[:]
+            heads = QK_HEADS // 2 if s == T_BLOCKS * ROUNDS - 1 else QK_HEADS
+            for head in range(0, QK_HEADS, heads):
+                part = slice(head, head + heads)
+                engine.tensor_tensor(
+                    out=sums[:, part, i - first, :],
+                    in0=with_cos[:, part].rearrange("p h j e -> p h (j e)"),
+                    in1=with_sin[:, part].rearrange("p h j e -> p h (j e)"),
+                    op=ALU.add,
                 )
+                if i == first + count - 1:
+                    out_head = QK_HEADS * (r % 2) + head
+                    nc.sync.dma_start(
+                        out=out_views[r // 2][:, out_head : out_head + heads, first : first + count, :],
+                        in_=sums[:, part],
+                    )
 
         def v_store_group(r, i):
             if r < ROUNDS - 1 or i < 4:
@@ -310,7 +336,7 @@ def tile_mimistreamingmultiheadattention_pa_kernel(tc, query, in_proj_w, out_0, 
             if i == first:
                 staged["v"] = v_stage.tile([P, heads, count, HEAD], F32, tag="v_stage", name="v_stage%d" % s)
             accv = pool.tile([P, V_COLS[r]], F32, tag=pool_tag, name="accv%d" % s)
-            multiply(accv[:], i, "v", r)
+            multiply(accv[:], i, "v", r, slice(0, V_COLS[r]))
             nc.scalar.copy(out=staged["v"][:, :, i - first, :], in_=accv[:].rearrange("p (h d) -> p h d", h=heads))
             if i == first + count - 1:
                 head = V_FIRST[r] // HEAD
@@ -324,24 +350,22 @@ def tile_mimistreamingmultiheadattention_pa_kernel(tc, query, in_proj_w, out_0, 
                 quantise_part("w", 0, g, slice(P * b, P * b + P))
 
         transpose_rows("w", 0, 0, scalar_copy)
-        cos_table(slice(0, 2))
-        transpose_query(0, 1, scalar_copy)
+        transpose_query(0, 1, vector_copy)
         quantise_first(0)
         quantise_query(0, 1)
         transpose_rows("w", 0, 1, scalar_copy)
-        sin_table(slice(0, 2))
         quantise_first(1)
-        transpose_rows("w", 0, 2, scalar_copy)
+        transpose_rows("w", 0, 2, vector_copy)
+        cos_table(slice(0, 2))
+        sin_table(slice(0, 2))
         transpose_rows("w", 0, 3, scalar_copy)
         quantise_first(2)
         transpose_query(1, 1, scalar_copy)
         quantise_first(3)
         transpose_query(2, 1, scalar_copy)
-        quantise_query(1, 1)
         multiply_qk(0)
-        quantise_query(2, 1)
-        cos_table(slice(2, T_BLOCKS))
-        sin_table(slice(2, T_BLOCKS))
+        quantise_query(1, 1)
+        rotate(0)
 
         to_transpose = {
             0: [("q", 3, 2)],
@@ -358,6 +382,7 @@ def tile_mimistreamingmultiheadattention_pa_kernel(tc, query, in_proj_w, out_0, 
             20: [("v", 3, 0), ("v", 3, 1)],
         }
         to_quantise = {
+            0: [("q", 2, 1)],
             1: [("q", 3, 2)],
             3: [("q", 5, 2)],
             5: [("q", 7, 1), ("w", 1)],
@@ -369,31 +394,36 @@ def tile_mimistreamingmultiheadattention_pa_kernel(tc, query, in_proj_w, out_0, 
         }
 
         last = T_BLOCKS * ROUNDS - 1
-        terms = {}
         for s in range(last + 1):
             for item in to_transpose.get(s + 1, []):
                 if item[0] != "q" and item[1] >= 2:
                     order_words(*item)
-            if s < last:
+            if 1 <= s + 1 <= last:
                 multiply_qk(s + 1)
             for item in to_transpose.get(s, []):
                 if item[0] == "q":
                     transpose_query(item[1], item[2], scalar_copy)
                 else:
                     transpose_rows(item[0], item[1], item[2], scalar_copy)
-            terms[s] = rotate(s)
-            if s in (6, 9, 12, 15, 18, 21, 24, 27,) :
-                add(s, nc.gpsimd, *terms[s])
+            if s == 0:
+                cos_table(slice(2, 4))
+                sin_table(slice(2, 4))
+            if s == 1:
+                cos_table(slice(4, T_BLOCKS))
+                sin_table(slice(4, T_BLOCKS))
+            if s >= 1:
+                rotate(s)
+            if s in (6, 9, 12, 15, 18, 21, 24, 27,):
+                add(s, nc.gpsimd)
+            for b in {1: [0], 3: [2], 5: [4], 8: [7], 11: [10], 14: [13], 17: [16], 20: [19], 23: [22], 26: [25], 29: [28], 30: [30], 31: [31]}.get(s, []):
+                add(b, nc.vector)
+            for item in to_quantise.get(s, []):
+                if item[0] == "q":
+                    quantise_query(item[1], item[2])
+                else:
+                    quantise_rows(*item)
             if s in (1, 3, 5, 8, 11, 14, 17, 20, 23, 26, 29,):
-                for item in to_quantise.get(s, []):
-                    if item[0] == "q":
-                        quantise_query(item[1], item[2])
-                    else:
-                        quantise_rows(*item)
-                add(s - 1, nc.vector, *terms[s - 1])
-                add(s, nc.gpsimd, *terms[s])
-            if s == last - 1 or s == last:
-                add(s, nc.vector, *terms[s])
+                add(s, nc.gpsimd)
             r, i = divmod(s, T_BLOCKS)
             for v_block in ((2 * i, 2 * i + 1) if r == ROUNDS - 1 else (i,)) if r and i * (r // 3) < 4 else ():
                 project_v(r, v_block, *((tp_pool, "tp") if r >= 2 else (accv_pool, "accv")))

@@ -46,7 +46,7 @@ def tile_mimistreamingmultiheadattention_pa_kernel(tc, query, in_proj_w, out_0, 
         order_pool = ctx.enter_context(tc.tile_pool(name="order", bufs=4))
         work = ctx.enter_context(tc.tile_pool(name="work", bufs=4))
         stage = ctx.enter_context(tc.tile_pool(name="stage", bufs=4))
-        v_stage = ctx.enter_context(tc.tile_pool(name="v_stage", bufs=3))
+        v_stage = ctx.enter_context(tc.tile_pool(name="v_stage", bufs=2))
         tp_pool = ctx.enter_context(tc.psum_pool(name="tp", bufs=4))
         acc_pool = ctx.enter_context(tc.psum_pool(name="acc", bufs=3))
         accv_pool = ctx.enter_context(tc.psum_pool(name="accv", bufs=1))
@@ -97,68 +97,84 @@ def tile_mimistreamingmultiheadattention_pa_kernel(tc, query, in_proj_w, out_0, 
         pos_int = const.tile([P, T_BLOCKS], I32)
         nc.gpsimd.iota(pos_int[:], pattern=[[1, T_BLOCKS]], base=0, channel_multiplier=T_BLOCKS)
 
-        signed_freq = const.tile([P, PAIRS, 2], F32)
-        nc.vector.memset(signed_freq[:, 0:1, 0:1], -1.0)
-        nc.vector.memset(signed_freq[:, 0:1, 1:2], 1.0)
+        freq = const.tile([P, PAIRS], F32)
+        nc.vector.memset(freq[:, 0:1], 1.0)
         warm = const.tile([P, 1], F32)
         nc.vector.memset(warm[:], 0.0)
         nc.scalar.activation(out=warm[:], in_=warm[:], func=ACT.Sin)
         for doubling in range(6):
             width = 2**doubling
             nc.vector.tensor_scalar(
-                out=signed_freq[:, width : 2 * width, :],
-                in0=signed_freq[:, 0:width, :],
+                out=freq[:, width : 2 * width],
+                in0=freq[:, 0:width],
                 scalar1=FREQ_RATIO**width,
                 scalar2=None,
                 op0=ALU.mult,
             )
+        signs = const.tile([P, 2], F32)
+        nc.vector.memset(signs[:, 0:1], 1.0)
+        nc.vector.memset(signs[:, 1:2], -1.0)
         pos = const.tile([P, T_BLOCKS], F32)
         nc.vector.tensor_copy(out=pos[:], in_=pos_int[:])
+
+        table_shape = [P, T_BLOCKS, PAIRS]
 
         def flat(tile_ap):
             return tile_ap.rearrange("p i j -> p (i j)")
 
-        signed_shape = [P, T_BLOCKS, HEAD]
-        turns = scratch.tile(signed_shape, F32)
+        turns = scratch.tile(table_shape, F32)
         nc.vector.scalar_tensor_tensor(
             out=turns[:],
-            in0=pos[:].unsqueeze(2).to_broadcast(signed_shape),
+            in0=pos[:].unsqueeze(2).to_broadcast(table_shape),
             scalar=1.0 / TWO_PI,
-            in1=signed_freq[:].rearrange("p j e -> p (j e)").unsqueeze(1).to_broadcast(signed_shape),
+            in1=freq[:].unsqueeze(1).to_broadcast(table_shape),
             op0=ALU.mult,
             op1=ALU.mult,
         )
-        back_sin = scratch.tile(signed_shape, F32)
+        near_sin = scratch.tile(table_shape, F32)
         nc.vector.tensor_scalar(
-            out=flat(back_sin[:]), in0=flat(turns[:]), scalar1=ROUND_MAGIC, scalar2=None, op0=ALU.add
+            out=flat(near_sin[:]), in0=flat(turns[:]), scalar1=ROUND_MAGIC, scalar2=None, op0=ALU.add
         )
-        quarter_on = turns[:].rearrange("p i (j e) -> p i j e", e=2)[:, :, :, 1]
-        back_cos = scratch.tile([P, T_BLOCKS, PAIRS], F32)
+        near_cos = scratch.tile(table_shape, F32)
         nc.vector.tensor_scalar(
-            out=back_cos[:], in0=quarter_on, scalar1=0.25, scalar2=ROUND_MAGIC, op0=ALU.add, op1=ALU.add
+            out=flat(near_cos[:]), in0=flat(turns[:]), scalar1=0.25, scalar2=ROUND_MAGIC, op0=ALU.add, op1=ALU.add
         )
+        back_sin = near_sin
         nc.vector.scalar_tensor_tensor(
-            out=flat(back_sin[:]), in0=flat(back_sin[:]), scalar=ROUND_MAGIC, in1=flat(turns[:]), op0=ALU.subtract, op1=ALU.subtract
+            out=flat(back_sin[:]), in0=flat(near_sin[:]), scalar=ROUND_MAGIC, in1=flat(turns[:]), op0=ALU.subtract, op1=ALU.subtract
         )
+        back_cos = near_cos
         nc.vector.scalar_tensor_tensor(
-            out=back_cos[:], in0=back_cos[:], scalar=ROUND_MAGIC, in1=quarter_on, op0=ALU.subtract, op1=ALU.subtract
+            out=flat(back_cos[:]), in0=flat(near_cos[:]), scalar=ROUND_MAGIC, in1=flat(turns[:]), op0=ALU.subtract, op1=ALU.subtract
         )
 
-        cos = const.tile(signed_shape, F32)
-        sin = const.tile(signed_shape, F32)
+        signed_back = scratch.tile([P, T_BLOCKS, PAIRS, 2], F32)
+        cos = const.tile([P, T_BLOCKS, PAIRS, 2], F32)
+        sin = const.tile([P, T_BLOCKS, PAIRS, 2], F32)
+
+        def sign_table(blocks):
+            shape = [P, blocks.stop - blocks.start, PAIRS, 2]
+            nc.vector.tensor_tensor(
+                out=signed_back[:, blocks],
+                in0=back_sin[:, blocks, :].unsqueeze(3).to_broadcast(shape),
+                in1=signs[:].unsqueeze(1).unsqueeze(1).to_broadcast(shape),
+                op=ALU.mult,
+            )
 
         def cos_table(blocks):
-            count = blocks.stop - blocks.start
+            shape = [P, blocks.stop - blocks.start, PAIRS, 2]
             nc.scalar.activation(
-                out=cos[:, blocks, :].rearrange("p i (j e) -> p i j e", e=2),
-                in_=back_cos[:, blocks, :].unsqueeze(3).to_broadcast([P, count, PAIRS, 2]),
+                out=cos[:, blocks],
+                in_=back_cos[:, blocks, :].unsqueeze(3).to_broadcast(shape),
                 func=ACT.Sin,
                 scale=-TWO_PI,
                 bias=math.pi / 2,
             )
 
         def sin_table(blocks):
-            nc.scalar.activation(out=sin[:, blocks, :], in_=back_sin[:, blocks, :], func=ACT.Sin, scale=-TWO_PI)
+            nc.scalar.activation(out=sin[:, blocks], in_=signed_back[:, blocks], func=ACT.Sin, scale=TWO_PI)
+
+        sign_table(slice(0, T_BLOCKS))
 
         def transpose_block(src_words, dst_words, copy):
             tp = tp_pool.tile([P, PASSES, 2, P], F32)
@@ -186,7 +202,7 @@ def tile_mimistreamingmultiheadattention_pa_kernel(tc, query, in_proj_w, out_0, 
 
         def transpose_query(first, count, copy):
             q_grouped[first] = grouped_pool.tile(
-                [P, count, PASSES, P, 4], BF16, tag="q_grouped", name="q_grouped%d" % first, align_bytes=64
+                [P, count, PASSES, P, 4], BF16, tag="q_grouped", name="q_grouped%d" % first, bufs=4, align_bytes=64
             )
             for n in range(count):
                 i = first + n
@@ -223,7 +239,7 @@ def tile_mimistreamingmultiheadattention_pa_kernel(tc, query, in_proj_w, out_0, 
                     BF16,
                     tag="%s_grouped" % kind,
                     name="%s_grouped%d" % (kind, r),
-                    bufs=2 if kind == "w" else 1,
+                    bufs=1,
                     align_bytes=64,
                 )
             dst = grouped[kind, r][:].bitcast(F32)[:, :, P * b : P * b + P, :]
@@ -239,12 +255,22 @@ def tile_mimistreamingmultiheadattention_pa_kernel(tc, query, in_proj_w, out_0, 
                 in_=grouped[kind, r][:].rearrange("p g c t -> p (g c t)"),
             )
 
-        def quantise_part(kind, r, g, cols):
-            nc.vector.quantize_mx(
-                out=codes[kind, r][:, g, cols].bitcast(FP8X4),
-                scales=scales[kind, r][:, g, cols],
-                in_=grouped[kind, r][:, g, cols, :].rearrange("p c t -> p (c t)"),
+        first_grouped = {}
+
+        def transpose_first(b, copy):
+            first_grouped[b] = grouped_pool.tile(
+                [P, PASSES, P, 4], BF16, tag="q_grouped", name="first_grouped%d" % b, bufs=4, align_bytes=64
             )
+            transpose_block(split_words(rows_sb["w", 0][:, b, :]), first_grouped[b][:].bitcast(F32), copy)
+
+        def quantise_first(b):
+            cols = slice(P * b, P * b + P)
+            for g in range(PASSES):
+                nc.vector.quantize_mx(
+                    out=codes["w", 0][:, g, cols].bitcast(FP8X4),
+                    scales=scales["w", 0][:, g, cols],
+                    in_=first_grouped[b][:, g].rearrange("p c t -> p (c t)"),
+                )
 
         def multiply(acc, i, kind, r, cols):
             for g in range(PASSES):
@@ -294,13 +320,13 @@ def tile_mimistreamingmultiheadattention_pa_kernel(tc, query, in_proj_w, out_0, 
                 nc.vector.tensor_tensor(
                     out=with_cos[:, part],
                     in0=pairs,
-                    in1=cos[:, i, :].rearrange("p (j e) -> p j e", e=2).unsqueeze(1).to_broadcast(shape),
+                    in1=cos[:, i].unsqueeze(1).to_broadcast(shape),
                     op=ALU.mult,
                 )
                 nc.vector.tensor_tensor(
                     out=with_sin[:, part],
                     in0=pairs[:, :, :, ::-1],
-                    in1=sin[:, i, :].rearrange("p (j e) -> p j e", e=2).unsqueeze(1).to_broadcast(shape),
+                    in1=sin[:, i].unsqueeze(1).to_broadcast(shape),
                     op=ALU.mult,
                 )
 
@@ -325,16 +351,23 @@ def tile_mimistreamingmultiheadattention_pa_kernel(tc, query, in_proj_w, out_0, 
                     )
 
         def v_store_group(r, i):
-            if r < ROUNDS - 1 or i < 4:
-                return i - i % 4, 4
-            return i - i % 2, 2
+            return i - i % 4, 4
+
+        def v_blocks(r, i):
+            if r == 0:
+                return ()
+            if r == 1:
+                return () if i == 0 else (i - 1, i) if i == T_BLOCKS - 1 else (i - 1,)
+            if r == ROUNDS - 1:
+                return (2 * i, 2 * i + 1) if i < T_BLOCKS // 2 else ()
+            return (i,)
 
         def project_v(r, i, pool, pool_tag):
             s = T_BLOCKS * r + i
             heads = V_COLS[r] // HEAD
             first, count = v_store_group(r, i)
             if i == first:
-                staged["v"] = v_stage.tile([P, heads, count, HEAD], F32, tag="v_stage", name="v_stage%d" % s)
+                staged["v"] = v_stage.tile([P, heads, count, HEAD], F32, tag="v_stage%d" % heads, name="v_stage%d" % s)
             accv = pool.tile([P, V_COLS[r]], F32, tag=pool_tag, name="accv%d" % s)
             multiply(accv[:], i, "v", r, slice(0, V_COLS[r]))
             nc.scalar.copy(out=staged["v"][:, :, i - first, :], in_=accv[:].rearrange("p (h d) -> p h d", h=heads))
@@ -345,21 +378,17 @@ def tile_mimistreamingmultiheadattention_pa_kernel(tc, query, in_proj_w, out_0, 
         scalar_copy = nc.scalar.copy
         vector_copy = nc.vector.tensor_copy
 
-        def quantise_first(b):
-            for g in range(PASSES):
-                quantise_part("w", 0, g, slice(P * b, P * b + P))
-
-        transpose_rows("w", 0, 0, scalar_copy)
-        transpose_query(0, 1, vector_copy)
+        transpose_first(0, scalar_copy)
+        transpose_query(0, 1, scalar_copy)
         quantise_first(0)
         quantise_query(0, 1)
-        transpose_rows("w", 0, 1, scalar_copy)
+        transpose_first(1, scalar_copy)
         quantise_first(1)
-        transpose_rows("w", 0, 2, vector_copy)
+        transpose_first(2, scalar_copy)
+        quantise_first(2)
+        transpose_first(3, scalar_copy)
         cos_table(slice(0, 2))
         sin_table(slice(0, 2))
-        transpose_rows("w", 0, 3, scalar_copy)
-        quantise_first(2)
         transpose_query(1, 1, scalar_copy)
         quantise_first(3)
         transpose_query(2, 1, scalar_copy)
@@ -425,5 +454,5 @@ def tile_mimistreamingmultiheadattention_pa_kernel(tc, query, in_proj_w, out_0, 
             if s in (1, 3, 5, 8, 11, 14, 17, 20, 23, 26, 29,):
                 add(s, nc.gpsimd)
             r, i = divmod(s, T_BLOCKS)
-            for v_block in ((2 * i, 2 * i + 1) if r == ROUNDS - 1 else (i,)) if r and i * (r // 3) < 4 else ():
+            for v_block in v_blocks(r, i):
                 project_v(r, v_block, *((tp_pool, "tp") if r >= 2 else (accv_pool, "accv")))

@@ -47,9 +47,8 @@ def tile_mimistreamingmultiheadattention_pa_kernel(tc, query, in_proj_w, out_0, 
         work = ctx.enter_context(tc.tile_pool(name="work", bufs=4))
         stage = ctx.enter_context(tc.tile_pool(name="stage", bufs=4))
         v_stage = ctx.enter_context(tc.tile_pool(name="v_stage", bufs=2))
-        tp_pool = ctx.enter_context(tc.psum_pool(name="tp", bufs=4))
+        tp_pool = ctx.enter_context(tc.psum_pool(name="tp", bufs=5))
         acc_pool = ctx.enter_context(tc.psum_pool(name="acc", bufs=3))
-        accv_pool = ctx.enter_context(tc.psum_pool(name="accv", bufs=1))
         ctx.enter_context(tc.manual_schedule())
 
         q_sb = loads.tile([P, T_BLOCKS, E], BF16)
@@ -64,15 +63,15 @@ def tile_mimistreamingmultiheadattention_pa_kernel(tc, query, in_proj_w, out_0, 
         def load_query(first, count):
             nc.sync.dma_start(out=q_sb[:, first : first + count, :], in_=q_rows[:, first : first + count, :])
 
-        def load_rows(dst, first_row, count):
-            rows = in_proj_w[first_row : first_row + count * P, :].rearrange("(b p) k -> p b k", p=P)
-            nc.sync.dma_start(out=dst, in_=rows)
-
         def load_w(r, first, count):
-            load_rows(w_sb[r][:, first : first + count, :], QK_COLS * r + P * first, count)
+            rows = in_proj_w[QK_COLS * r : QK_COLS * (r + 1), :].rearrange("(p b) k -> p b k", p=P)
+            blocks = slice(first, first + count)
+            nc.sync.dma_start(out=w_sb[r][:, blocks, :], in_=rows[:, blocks, :])
 
         def load_v(r):
-            load_rows(v_sb[r][:], 2 * E + V_FIRST[r], V_COLS[r] // P)
+            first_row = 2 * E + V_FIRST[r]
+            rows = in_proj_w[first_row : first_row + V_COLS[r], :].rearrange("(p b) k -> p b k", p=P)
+            nc.sync.dma_start(out=v_sb[r][:], in_=rows)
 
         load_w(0, 0, 1)
         load_query(0, 1)
@@ -82,15 +81,9 @@ def tile_mimistreamingmultiheadattention_pa_kernel(tc, query, in_proj_w, out_0, 
         load_query(1, 1)
         load_query(2, 2)
         load_query(4, 4)
-        load_w(1, 0, 2)
-        load_w(1, 2, 2)
-        load_v(1)
-        load_w(2, 0, 2)
-        load_w(2, 2, 2)
-        load_v(2)
-        load_w(3, 0, 2)
-        load_w(3, 2, 2)
-        load_v(3)
+        for r in range(1, ROUNDS):
+            load_w(r, 0, W_BLOCKS)
+            load_v(r)
 
         ident = const.tile([P, P], F32)
         make_identity(nc, ident[:])
@@ -288,11 +281,9 @@ def tile_mimistreamingmultiheadattention_pa_kernel(tc, query, in_proj_w, out_0, 
         accs = {}
         staged = {}
 
-        def multiply_qk(s, first_head=0, heads=QK_HEADS):
-            acc = acc_pool.tile([P, heads * HEAD], F32, tag="acc", name="acc%d_%d" % (s, first_head))
-            cols = slice(first_head * HEAD, (first_head + heads) * HEAD)
-            multiply(acc[:], s % T_BLOCKS, "w", s // T_BLOCKS, cols)
-            accs.setdefault(s, []).append((acc, first_head, heads))
+        def multiply_qk(s):
+            accs[s] = acc_pool.tile([P, QK_COLS], F32, tag="acc", name="acc%d" % s)
+            multiply(accs[s][:], s % T_BLOCKS, "w", s // T_BLOCKS, slice(0, QK_COLS))
 
         def store_group(r, i):
             if r < ROUNDS - 1 or i < 4:
@@ -313,22 +304,21 @@ def tile_mimistreamingmultiheadattention_pa_kernel(tc, query, in_proj_w, out_0, 
                 with_sin = work.tile([P, QK_HEADS, PAIRS, 2], F32, tag="with_sin", name="with_sin%d" % s)
                 terms[s] = (staged["qk"], with_cos, with_sin)
             sums, with_cos, with_sin = terms[s]
-            for acc, first_head, heads in accs.pop(s):
-                part = slice(first_head, first_head + heads)
-                shape = [P, heads, PAIRS, 2]
-                pairs = acc[:].rearrange("p (h j e) -> p h j e", h=heads, e=2)
-                nc.vector.tensor_tensor(
-                    out=with_cos[:, part],
-                    in0=pairs,
-                    in1=cos[:, i].unsqueeze(1).to_broadcast(shape),
-                    op=ALU.mult,
-                )
-                nc.vector.tensor_tensor(
-                    out=with_sin[:, part],
-                    in0=pairs[:, :, :, ::-1],
-                    in1=sin[:, i].unsqueeze(1).to_broadcast(shape),
-                    op=ALU.mult,
-                )
+            acc = accs.pop(s)
+            shape = [P, QK_HEADS, PAIRS // 2, 2, 2]
+            pairs = acc[:].rearrange("p (u e h r) -> p h r u e", u=2, e=2, h=QK_HEADS)
+            nc.vector.tensor_tensor(
+                out=with_cos[:].rearrange("p h (r u) e -> p h r u e", u=2),
+                in0=pairs,
+                in1=cos[:, i].rearrange("p (r u) e -> p r u e", u=2).unsqueeze(1).to_broadcast(shape),
+                op=ALU.mult,
+            )
+            nc.vector.tensor_tensor(
+                out=with_sin[:].rearrange("p h (r u) e -> p h r u e", u=2),
+                in0=pairs[:, :, :, :, ::-1],
+                in1=sin[:, i].rearrange("p (r u) e -> p r u e", u=2).unsqueeze(1).to_broadcast(shape),
+                op=ALU.mult,
+            )
 
         def add(s, engine):
             sums, with_cos, with_sin = terms[s]
@@ -370,7 +360,11 @@ def tile_mimistreamingmultiheadattention_pa_kernel(tc, query, in_proj_w, out_0, 
                 staged["v"] = v_stage.tile([P, heads, count, HEAD], F32, tag="v_stage%d" % heads, name="v_stage%d" % s)
             accv = pool.tile([P, V_COLS[r]], F32, tag=pool_tag, name="accv%d" % s)
             multiply(accv[:], i, "v", r, slice(0, V_COLS[r]))
-            nc.scalar.copy(out=staged["v"][:, :, i - first, :], in_=accv[:].rearrange("p (h d) -> p h d", h=heads))
+            blocks = V_COLS[r] // P
+            nc.scalar.copy(
+                out=staged["v"][:, :, i - first, :].rearrange("p h (r b) -> p h r b", b=blocks),
+                in_=accv[:].rearrange("p (b h r) -> p h r b", b=blocks, h=heads),
+            )
             if i == first + count - 1:
                 head = V_FIRST[r] // HEAD
                 nc.sync.dma_start(out=out_views[2][:, head : head + heads, first : i + 1, :], in_=staged["v"][:])
@@ -399,9 +393,10 @@ def tile_mimistreamingmultiheadattention_pa_kernel(tc, query, in_proj_w, out_0, 
         to_transpose = {
             0: [("q", 3, 2)],
             1: [("q", 5, 2)],
-            2: [("w", 1, 0), ("w", 1, 1)],
-            3: [("q", 7, 1), ("w", 1, 2), ("w", 1, 3)],
-            5: [("v", 1, 0), ("v", 1, 1)],
+            2: [("q", 7, 1), ("w", 1, 0)],
+            3: [("w", 1, 1), ("w", 1, 2)],
+            4: [("w", 1, 3)],
+            6: [("v", 1, 0), ("v", 1, 1)],
             7: [("w", 2, 0), ("w", 2, 1)],
             9: [("w", 2, 2), ("w", 2, 3)],
             11: [("v", 2, 0), ("v", 2, 1)],
@@ -455,4 +450,4 @@ def tile_mimistreamingmultiheadattention_pa_kernel(tc, query, in_proj_w, out_0, 
                 add(s, nc.gpsimd)
             r, i = divmod(s, T_BLOCKS)
             for v_block in v_blocks(r, i):
-                project_v(r, v_block, *((tp_pool, "tp") if r >= 2 else (accv_pool, "accv")))
+                project_v(r, v_block, tp_pool, "tp")

@@ -27,6 +27,7 @@ QK_HEADS = QK_COLS // HEAD
 W_BLOCKS = QK_COLS // P
 V_FIRST = [0, 0, 256, 768]
 V_COLS = [0, 256, 512, 256]
+WAKING_PRODUCTS = 4
 
 FLOPS = 2 * T * E * 3 * E
 
@@ -84,6 +85,14 @@ def tile_mimistreamingmultiheadattention_pa_kernel(tc, query, in_proj_w, out_0, 
         for r in range(1, ROUNDS):
             load_w(r, 0, W_BLOCKS)
             load_v(r)
+
+        zeros = const.tile([P, QK_COLS // 2], F32)
+        nc.gpsimd.memset(zeros[:], 0.0)
+        for n in range(WAKING_PRODUCTS):
+            nothing = acc_pool.tile([P, QK_COLS], F32, tag="acc", name="nothing%d" % n)
+            nc.tensor.matmul(
+                nothing[:], lhsT=zeros[:].bitcast(BF16)[:, 0:P], rhs=zeros[:].bitcast(BF16), start=True, stop=True
+            )
 
         ident = const.tile([P, P], F32)
         make_identity(nc, ident[:])
@@ -167,7 +176,7 @@ def tile_mimistreamingmultiheadattention_pa_kernel(tc, query, in_proj_w, out_0, 
         def sin_table(blocks):
             nc.scalar.activation(out=sin[:, blocks], in_=signed_back[:, blocks], func=ACT.Sin, scale=TWO_PI)
 
-        sign_table(slice(0, T_BLOCKS))
+        sign_table(slice(0, 2))
 
         def transpose_block(src_words, dst_words, copy):
             tp = tp_pool.tile([P, PASSES, 2, P], F32)
@@ -286,61 +295,60 @@ def tile_mimistreamingmultiheadattention_pa_kernel(tc, query, in_proj_w, out_0, 
             multiply(accs[s][:], s % T_BLOCKS, "w", s // T_BLOCKS, slice(0, QK_COLS))
 
         def store_group(r, i):
-            if r < ROUNDS - 1 or i < 4:
+            if r < 2 or (r == 2 and i < 4):
                 return i - i % 4, 4
-            if i < 6:
-                return 4, 2
+            if r == 2 or i < 6:
+                return i - i % 2, 2
             return i, 1
 
         terms = {}
 
-        def rotate(s):
+        def rotate(s, first_head=0, heads=QK_HEADS):
             r, i = divmod(s, T_BLOCKS)
-            first, count = store_group(r, i)
-            if i == first and s not in terms:
-                staged["qk"] = stage.tile([P, QK_HEADS, count, HEAD], F32, tag="qk_stage", name="qk_stage%d" % s)
-            if s not in terms:
+            if first_head == 0:
+                first, count = store_group(r, i)
+                if i == first:
+                    staged["qk"] = stage.tile([P, QK_HEADS, count, HEAD], F32, tag="qk_stage", name="qk_stage%d" % s)
                 with_cos = work.tile([P, QK_HEADS, PAIRS, 2], F32, tag="with_cos", name="with_cos%d" % s)
                 with_sin = work.tile([P, QK_HEADS, PAIRS, 2], F32, tag="with_sin", name="with_sin%d" % s)
                 terms[s] = (staged["qk"], with_cos, with_sin)
             sums, with_cos, with_sin = terms[s]
-            acc = accs.pop(s)
-            shape = [P, QK_HEADS, PAIRS // 2, 2, 2]
-            pairs = acc[:].rearrange("p (u e h r) -> p h r u e", u=2, e=2, h=QK_HEADS)
+            part = slice(first_head, first_head + heads)
+            shape = [P, heads, PAIRS // 2, 2, 2]
+            pairs = accs[s][:].rearrange("p (u e h r) -> p h r u e", u=2, e=2, h=QK_HEADS)[:, part]
             nc.vector.tensor_tensor(
-                out=with_cos[:].rearrange("p h (r u) e -> p h r u e", u=2),
+                out=with_cos[:, part].rearrange("p h (r u) e -> p h r u e", u=2),
                 in0=pairs,
                 in1=cos[:, i].rearrange("p (r u) e -> p r u e", u=2).unsqueeze(1).to_broadcast(shape),
                 op=ALU.mult,
             )
             nc.vector.tensor_tensor(
-                out=with_sin[:].rearrange("p h (r u) e -> p h r u e", u=2),
+                out=with_sin[:, part].rearrange("p h (r u) e -> p h r u e", u=2),
                 in0=pairs[:, :, :, :, ::-1],
                 in1=sin[:, i].rearrange("p (r u) e -> p r u e", u=2).unsqueeze(1).to_broadcast(shape),
                 op=ALU.mult,
             )
 
-        def add(s, engine):
+        def add(s, engine, first_head=0, heads=QK_HEADS):
             sums, with_cos, with_sin = terms[s]
             r, i = divmod(s, T_BLOCKS)
             first, count = store_group(r, i)
-            heads = QK_HEADS // 2 if s == T_BLOCKS * ROUNDS - 1 else QK_HEADS
-            for head in range(0, QK_HEADS, heads):
-                part = slice(head, head + heads)
-                engine.tensor_tensor(
-                    out=sums[:, part, i - first, :],
-                    in0=with_cos[:, part].rearrange("p h j e -> p h (j e)"),
-                    in1=with_sin[:, part].rearrange("p h j e -> p h (j e)"),
-                    op=ALU.add,
+            part = slice(first_head, first_head + heads)
+            engine.tensor_tensor(
+                out=sums[:, part, i - first, :],
+                in0=with_cos[:, part].rearrange("p h j e -> p h (j e)"),
+                in1=with_sin[:, part].rearrange("p h j e -> p h (j e)"),
+                op=ALU.add,
+            )
+            if i == first + count - 1:
+                head = QK_HEADS * (r % 2) + first_head
+                nc.sync.dma_start(
+                    out=out_views[r // 2][:, head : head + heads, first : first + count, :], in_=sums[:, part]
                 )
-                if i == first + count - 1:
-                    out_head = QK_HEADS * (r % 2) + head
-                    nc.sync.dma_start(
-                        out=out_views[r // 2][:, out_head : out_head + heads, first : first + count, :],
-                        in_=sums[:, part],
-                    )
 
         def v_store_group(r, i):
+            if r == 2 and i >= 4:
+                return i - i % 2, 2
             return i - i % 4, 4
 
         def v_blocks(r, i):
@@ -357,7 +365,13 @@ def tile_mimistreamingmultiheadattention_pa_kernel(tc, query, in_proj_w, out_0, 
             heads = V_COLS[r] // HEAD
             first, count = v_store_group(r, i)
             if i == first:
-                staged["v"] = v_stage.tile([P, heads, count, HEAD], F32, tag="v_stage%d" % heads, name="v_stage%d" % s)
+                staged["v"] = v_stage.tile(
+                    [P, heads, count, HEAD],
+                    F32,
+                    tag="v_stage%d_%d" % (heads, count),
+                    name="v_stage%d" % s,
+                    bufs=1 if heads * count == 16 else 2,
+                )
             accv = pool.tile([P, V_COLS[r]], F32, tag=pool_tag, name="accv%d" % s)
             multiply(accv[:], i, "v", r, slice(0, V_COLS[r]))
             blocks = V_COLS[r] // P
@@ -386,6 +400,7 @@ def tile_mimistreamingmultiheadattention_pa_kernel(tc, query, in_proj_w, out_0, 
         transpose_query(1, 1, scalar_copy)
         quantise_first(3)
         transpose_query(2, 1, scalar_copy)
+        sign_table(slice(2, T_BLOCKS))
         multiply_qk(0)
         quantise_query(1, 1)
         rotate(0)
@@ -418,7 +433,7 @@ def tile_mimistreamingmultiheadattention_pa_kernel(tc, query, in_proj_w, out_0, 
         }
 
         last = T_BLOCKS * ROUNDS - 1
-        for s in range(last + 1):
+        for s in range(last):
             for item in to_transpose.get(s + 1, []):
                 if item[0] != "q" and item[1] >= 2:
                     order_words(*item)
@@ -439,7 +454,7 @@ def tile_mimistreamingmultiheadattention_pa_kernel(tc, query, in_proj_w, out_0, 
                 rotate(s)
             if s in (6, 9, 12, 15, 18, 21, 24, 27,):
                 add(s, nc.gpsimd)
-            for b in {1: [0], 3: [2], 5: [4], 8: [7], 11: [10], 14: [13], 17: [16], 20: [19], 23: [22], 26: [25], 29: [28], 30: [30], 31: [31]}.get(s, []):
+            for b in {1: [0], 3: [2], 5: [4], 8: [7], 11: [10], 14: [13], 17: [16], 20: [19], 23: [22], 26: [25], 29: [28]}.get(s, []):
                 add(b, nc.vector)
             for item in to_quantise.get(s, []):
                 if item[0] == "q":
@@ -451,3 +466,10 @@ def tile_mimistreamingmultiheadattention_pa_kernel(tc, query, in_proj_w, out_0, 
             r, i = divmod(s, T_BLOCKS)
             for v_block in v_blocks(r, i):
                 project_v(r, v_block, tp_pool, "tp")
+
+        half = QK_HEADS // 2
+        rotate(last, 0, half)
+        add(last - 1, nc.vector)
+        rotate(last, half, half)
+        add(last, nc.vector, 0, half)
+        add(last, nc.vector, half, half)

import math
from contextlib import ExitStack

import concourse.mybir as mybir
from concourse.masks import make_identity

F32 = mybir.dt.float32
BF16 = mybir.dt.bfloat16
I32 = mybir.dt.int32
U32 = mybir.dt.uint32
U8 = mybir.dt.uint8
FP8X4 = mybir.dt.float8_e4m3fn_x4
ALU = mybir.AluOpType
ACT = mybir.ActivationFunctionType

P = 128
T = 1024
E = 1024
HEAD = 128
PAIRS = HEAD // 2
K_PASS = 4 * P
PASSES = E // K_PASS
T_BLOCKS = T // P
ROUNDS = 4
QK_COLS = 512
QK_HEADS = QK_COLS // HEAD
W_BLOCKS = QK_COLS // P
V_FIRST = [0, 0, 256, 768]
V_COLS = [0, 256, 512, 256]
WAKING_PRODUCTS = 4

FLOPS = 2 * T * E * 3 * E

FREQ_RATIO = math.exp(-math.log(10000.0) * 2.0 / HEAD)
TWO_PI = 2.0 * math.pi
ROUND_MAGIC = 1.5 * 2.0**23


def tile_mimistreamingmultiheadattention_pa_kernel(tc, query, in_proj_w, out_0, out_1, out_2):
    nc = tc.nc
    with ExitStack() as ctx:
        const = ctx.enter_context(tc.tile_pool(name="const", bufs=1))
        scratch = ctx.enter_context(tc.tile_pool(name="scratch", bufs=1))
        loads = ctx.enter_context(tc.tile_pool(name="loads", bufs=1))
        grouped_pool = ctx.enter_context(tc.tile_pool(name="grouped", bufs=2))
        mx = ctx.enter_context(tc.tile_pool(name="mx", bufs=1))
        order_pool = ctx.enter_context(tc.tile_pool(name="order", bufs=4))
        work = ctx.enter_context(tc.tile_pool(name="work", bufs=4))
        stage = ctx.enter_context(tc.tile_pool(name="stage", bufs=4))
        v_stage = ctx.enter_context(tc.tile_pool(name="v_stage", bufs=2))
        tp_pool = ctx.enter_context(tc.psum_pool(name="tp", bufs=5))
        acc_pool = ctx.enter_context(tc.psum_pool(name="acc", bufs=3))
        ctx.enter_context(tc.manual_schedule())

        q_sb = loads.tile([P, T_BLOCKS, E], BF16)
        q_rows = query.rearrange("b (p i) k -> p (b i) k", i=T_BLOCKS)
        w_sb = {}
        v_sb = {}
        for r in range(ROUNDS):
            w_sb[r] = loads.tile([P, W_BLOCKS, E], BF16, name="w_sb%d" % r)
            if V_COLS[r]:
                v_sb[r] = loads.tile([P, V_COLS[r] // P, E], BF16, name="v_sb%d" % r)

        def load_query(first, count):
            nc.sync.dma_start(out=q_sb[:, first : first + count, :], in_=q_rows[:, first : first + count, :])

        def load_w(r, first, count):
            rows = in_proj_w[QK_COLS * r : QK_COLS * (r + 1), :].rearrange("(p b) k -> p b k", p=P)
            blocks = slice(first, first + count)
            nc.sync.dma_start(out=w_sb[r][:, blocks, :], in_=rows[:, blocks, :])

        def load_v(r):
            first_row = 2 * E + V_FIRST[r]
            rows = in_proj_w[first_row : first_row + V_COLS[r], :].rearrange("(p b) k -> p b k", p=P)
            nc.sync.dma_start(out=v_sb[r][:], in_=rows)

        load_w(0, 0, 1)
        load_query(0, 1)
        load_w(0, 1, 1)
        load_w(0, 2, 1)
        load_w(0, 3, 1)
        load_query(1, 1)
        load_query(2, 2)
        load_query(4, 4)
        for r in range(1, ROUNDS):
            load_w(r, 0, W_BLOCKS)
            load_v(r)

        zeros = const.tile([P, QK_COLS // 2], F32)
        nc.gpsimd.memset(zeros[:], 0.0)
        for n in range(WAKING_PRODUCTS):
            nothing = acc_pool.tile([P, QK_COLS], F32, tag="acc", name="nothing%d" % n)
            nc.tensor.matmul(
                nothing[:], lhsT=zeros[:].bitcast(BF16)[:, 0:P], rhs=zeros[:].bitcast(BF16), start=True, stop=True
            )

        ident = const.tile([P, P], F32)
        make_identity(nc, ident[:])
        pos_int = const.tile([P, T_BLOCKS], I32)
        nc.gpsimd.iota(pos_int[:], pattern=[[1, T_BLOCKS]], base=0, channel_multiplier=T_BLOCKS)

        freq = const.tile([P, PAIRS], F32)
        nc.vector.memset(freq[:, 0:1], 1.0)
        warm = const.tile([P, 1], F32)
        nc.vector.memset(warm[:], 0.0)
        nc.scalar.activation(out=warm[:], in_=warm[:], func=ACT.Sin)
        for doubling in range(6):
            width = 2**doubling
            nc.vector.tensor_scalar(
                out=freq[:, width : 2 * width],
                in0=freq[:, 0:width],
                scalar1=FREQ_RATIO**width,
                scalar2=None,
                op0=ALU.mult,
            )
        signs = const.tile([P, 2], F32)
        nc.vector.memset(signs[:, 0:1], 1.0)
        nc.vector.memset(signs[:, 1:2], -1.0)
        pos = const.tile([P, T_BLOCKS], F32)
        nc.vector.tensor_copy(out=pos[:], in_=pos_int[:])

        table_shape = [P, T_BLOCKS, PAIRS]

        def flat(tile_ap):
            return tile_ap.rearrange("p i j -> p (i j)")

        turns = scratch.tile(table_shape, F32)
        nc.vector.scalar_tensor_tensor(
            out=turns[:],
            in0=pos[:].unsqueeze(2).to_broadcast(table_shape),
            scalar=1.0 / TWO_PI,
            in1=freq[:].unsqueeze(1).to_broadcast(table_shape),
            op0=ALU.mult,
            op1=ALU.mult,
        )
        near_sin = scratch.tile(table_shape, F32)
        nc.vector.tensor_scalar(
            out=flat(near_sin[:]), in0=flat(turns[:]), scalar1=ROUND_MAGIC, scalar2=None, op0=ALU.add
        )
        near_cos = scratch.tile(table_shape, F32)
        nc.vector.tensor_scalar(
            out=flat(near_cos[:]), in0=flat(turns[:]), scalar1=0.25, scalar2=ROUND_MAGIC, op0=ALU.add, op1=ALU.add
        )
        back_sin = near_sin
        nc.vector.scalar_tensor_tensor(
            out=flat(back_sin[:]), in0=flat(near_sin[:]), scalar=ROUND_MAGIC, in1=flat(turns[:]), op0=ALU.subtract, op1=ALU.subtract
        )
        back_cos = near_cos
        nc.vector.scalar_tensor_tensor(
            out=flat(back_cos[:]), in0=flat(near_cos[:]), scalar=ROUND_MAGIC, in1=flat(turns[:]), op0=ALU.subtract, op1=ALU.subtract
        )

        signed_back = scratch.tile([P, T_BLOCKS, PAIRS, 2], F32)
        cos = const.tile([P, T_BLOCKS, PAIRS, 2], F32)
        sin = const.tile([P, T_BLOCKS, PAIRS, 2], F32)

        def sign_table(blocks):
            shape = [P, blocks.stop - blocks.start, PAIRS, 2]
            nc.vector.tensor_tensor(
                out=signed_back[:, blocks],
                in0=back_sin[:, blocks, :].unsqueeze(3).to_broadcast(shape),
                in1=signs[:].unsqueeze(1).unsqueeze(1).to_broadcast(shape),
                op=ALU.mult,
            )

        def cos_table(blocks):
            shape = [P, blocks.stop - blocks.start, PAIRS, 2]
            nc.scalar.activation(
                out=cos[:, blocks],
                in_=back_cos[:, blocks, :].unsqueeze(3).to_broadcast(shape),
                func=ACT.Sin,
                scale=-TWO_PI,
                bias=math.pi / 2,
            )

        def sin_table(blocks):
            nc.scalar.activation(out=sin[:, blocks], in_=signed_back[:, blocks], func=ACT.Sin, scale=TWO_PI)

        sign_table(slice(0, 2))

        def transpose_block(src_words, dst_words, copy):
            tp = tp_pool.tile([P, PASSES, 2, P], F32)
            for g in range(PASSES):
                for u in range(2):
                    nc.tensor.transpose(tp[:, g, u, :], src_words[:, g, u, :], ident[:])
            copy(out=dst_words, in_=tp[:].rearrange("p g u r -> p g r u"))

        def split_words(rows):
            return rows.bitcast(F32).rearrange("p (g w u) -> p g u w", g=PASSES, u=2)

        ordered = {}

        def order_words(kind, r, b, copy=nc.scalar.copy):
            if kind == "q":
                rows = q_sb[:, b, :]
            else:
                rows = rows_sb[kind, r][:, b, :]
            ordered[kind, r, b] = order_pool.tile([P, PASSES, 2, P], F32, tag="ordered", name="ordered_%s%d%d" % (kind, r, b))
            copy(out=ordered[kind, r, b][:], in_=split_words(rows))

        q_codes = mx.tile([P, T_BLOCKS, PASSES, P], U32, align_bytes=64)
        q_scales = mx.tile([P, T_BLOCKS, PASSES, P], U8, align_bytes=64)
        q_grouped = {}

        def transpose_query(first, count, copy):
            q_grouped[first] = grouped_pool.tile(
                [P, count, PASSES, P, 4], BF16, tag="q_grouped", name="q_grouped%d" % first, bufs=4, align_bytes=64
            )
            for n in range(count):
                i = first + n
                if ("q", 0, i) in ordered:
                    words = ordered["q", 0, i][:]
                else:
                    words = split_words(q_sb[:, i, :])
                transpose_block(words, q_grouped[first][:].bitcast(F32)[:, n], copy)

        def quantise_query(first, count):
            blocks = slice(first, first + count)
            nc.vector.quantize_mx(
                out=q_codes[:, blocks].rearrange("p i g c -> p (i g c)").bitcast(FP8X4),
                scales=q_scales[:, blocks].rearrange("p i g c -> p (i g c)"),
                in_=q_grouped[first][:].rearrange("p i g c t -> p (i g c t)"),
            )

        rows_sb = {}
        grouped = {}
        codes = {}
        scales = {}
        for r in range(ROUNDS):
            for kind, source, cols in (("w", w_sb, QK_COLS), ("v", v_sb, V_COLS[r])):
                if cols:
                    rows_sb[kind, r] = source[r]
                    codes[kind, r] = mx.tile([P, PASSES, cols], U32, name="%s_codes%d" % (kind, r), align_bytes=64)
                    scales[kind, r] = mx.tile([P, PASSES, cols], U8, name="%s_scales%d" % (kind, r), align_bytes=64)

        def transpose_rows(kind, r, b, copy):
            if b == 0:
                cols = QK_COLS if kind == "w" else V_COLS[r]
                grouped[kind, r] = grouped_pool.tile(
                    [P, PASSES, cols, 4],
                    BF16,
                    tag="%s_grouped" % kind,
                    name="%s_grouped%d" % (kind, r),
                    bufs=1,
                    align_bytes=64,
                )
            dst = grouped[kind, r][:].bitcast(F32)[:, :, P * b : P * b + P, :]
            if (kind, r, b) in ordered:
                transpose_block(ordered[kind, r, b][:], dst, copy)
            else:
                transpose_block(split_words(rows_sb[kind, r][:, b, :]), dst, copy)

        def quantise_rows(kind, r):
            nc.vector.quantize_mx(
                out=codes[kind, r][:].rearrange("p g c -> p (g c)").bitcast(FP8X4),
                scales=scales[kind, r][:].rearrange("p g c -> p (g c)"),
                in_=grouped[kind, r][:].rearrange("p g c t -> p (g c t)"),
            )

        first_grouped = {}

        def transpose_first(b, copy):
            first_grouped[b] = grouped_pool.tile(
                [P, PASSES, P, 4], BF16, tag="q_grouped", name="first_grouped%d" % b, bufs=4, align_bytes=64
            )
            transpose_block(split_words(rows_sb["w", 0][:, b, :]), first_grouped[b][:].bitcast(F32), copy)

        def quantise_first(b):
            cols = slice(P * b, P * b + P)
            for g in range(PASSES):
                nc.vector.quantize_mx(
                    out=codes["w", 0][:, g, cols].bitcast(FP8X4),
                    scales=scales["w", 0][:, g, cols],
                    in_=first_grouped[b][:, g].rearrange("p c t -> p (c t)"),
                )

        def multiply(acc, i, kind, r, cols):
            for g in range(PASSES):
                nc.tensor.matmul_mx(
                    out=acc,
                    lhsT=q_codes[:, i, g, :].bitcast(FP8X4),
                    lhsT_scale=q_scales[:, i, g, :],
                    rhs=codes[kind, r][:, g, cols].bitcast(FP8X4),
                    rhs_scale=scales[kind, r][:, g, cols],
                    start=(g == 0),
                    stop=(g == PASSES - 1),
                )

        out_views = [o.rearrange("b h (p i) d -> p (b h) i d", i=T_BLOCKS) for o in (out_0, out_1, out_2)]
        accs = {}
        staged = {}

        def multiply_qk(s):
            accs[s] = acc_pool.tile([P, QK_COLS], F32, tag="acc", name="acc%d" % s)
            multiply(accs[s][:], s % T_BLOCKS, "w", s // T_BLOCKS, slice(0, QK_COLS))

        def store_group(r, i):
            if r < 2 or (r == 2 and i < 4):
                return i - i % 4, 4
            if r == 2 or i < 6:
                return i - i % 2, 2
            return i, 1

        terms = {}

        def rotate(s, first_head=0, heads=QK_HEADS):
            r, i = divmod(s, T_BLOCKS)
            if first_head == 0:
                first, count = store_group(r, i)
                if i == first:
                    staged["qk"] = stage.tile([P, QK_HEADS, count, HEAD], F32, tag="qk_stage", name="qk_stage%d" % s)
                with_cos = work.tile([P, QK_HEADS, PAIRS, 2], F32, tag="with_cos", name="with_cos%d" % s)
                with_sin = work.tile([P, QK_HEADS, PAIRS, 2], F32, tag="with_sin", name="with_sin%d" % s)
                terms[s] = (staged["qk"], with_cos, with_sin)
            sums, with_cos, with_sin = terms[s]
            part = slice(first_head, first_head + heads)
            shape = [P, heads, PAIRS // 2, 2, 2]
            pairs = accs[s][:].rearrange("p (u e h r) -> p h r u e", u=2, e=2, h=QK_HEADS)[:, part]
            nc.vector.tensor_tensor(
                out=with_cos[:, part].rearrange("p h (r u) e -> p h r u e", u=2),
                in0=pairs,
                in1=cos[:, i].rearrange("p (r u) e -> p r u e", u=2).unsqueeze(1).to_broadcast(shape),
                op=ALU.mult,
            )
            nc.vector.tensor_tensor(
                out=with_sin[:, part].rearrange("p h (r u) e -> p h r u e", u=2),
                in0=pairs[:, :, :, :, ::-1],
                in1=sin[:, i].rearrange("p (r u) e -> p r u e", u=2).unsqueeze(1).to_broadcast(shape),
                op=ALU.mult,
            )

        def add(s, engine, first_head=0, heads=QK_HEADS):
            sums, with_cos, with_sin = terms[s]
            r, i = divmod(s, T_BLOCKS)
            first, count = store_group(r, i)
            part = slice(first_head, first_head + heads)
            engine.tensor_tensor(
                out=sums[:, part, i - first, :],
                in0=with_cos[:, part].rearrange("p h j e -> p h (j e)"),
                in1=with_sin[:, part].rearrange("p h j e -> p h (j e)"),
                op=ALU.add,
            )
            if i == first + count - 1:
                head = QK_HEADS * (r % 2) + first_head
                nc.sync.dma_start(
                    out=out_views[r // 2][:, head : head + heads, first : first + count, :], in_=sums[:, part]
                )

        def v_store_group(r, i):
            if r == 2 and i >= 4:
                return i - i % 2, 2
            return i - i % 4, 4

        def v_blocks(r, i):
            if r == 0:
                return ()
            if r == 1:
                return () if i == 0 else (i - 1, i) if i == T_BLOCKS - 1 else (i - 1,)
            if r == ROUNDS - 1:
                return (2 * i, 2 * i + 1) if i < T_BLOCKS // 2 else ()
            return (i,)

        def project_v(r, i, pool, pool_tag):
            s = T_BLOCKS * r + i
            heads = V_COLS[r] // HEAD
            first, count = v_store_group(r, i)
            if i == first:
                staged["v"] = v_stage.tile(
                    [P, heads, count, HEAD],
                    F32,
                    tag="v_stage%d_%d" % (heads, count),
                    name="v_stage%d" % s,
                    bufs=1 if heads * count == 16 else 2,
                )
            accv = pool.tile([P, V_COLS[r]], F32, tag=pool_tag, name="accv%d" % s)
            multiply(accv[:], i, "v", r, slice(0, V_COLS[r]))
            blocks = V_COLS[r] // P
            nc.scalar.copy(
                out=staged["v"][:, :, i - first, :].rearrange("p h (r b) -> p h r b", b=blocks),
                in_=accv[:].rearrange("p (b h r) -> p h r b", b=blocks, h=heads),
            )
            if i == first + count - 1:
                head = V_FIRST[r] // HEAD
                nc.sync.dma_start(out=out_views[2][:, head : head + heads, first : i + 1, :], in_=staged["v"][:])

        scalar_copy = nc.scalar.copy
        vector_copy = nc.vector.tensor_copy

        transpose_first(0, scalar_copy)
        transpose_query(0, 1, scalar_copy)
        quantise_first(0)
        quantise_query(0, 1)
        transpose_first(1, scalar_copy)
        quantise_first(1)
        transpose_first(2, scalar_copy)
        quantise_first(2)
        transpose_first(3, scalar_copy)
        cos_table(slice(0, 2))
        sin_table(slice(0, 2))
        transpose_query(1, 1, scalar_copy)
        quantise_first(3)
        transpose_query(2, 1, scalar_copy)
        sign_table(slice(2, T_BLOCKS))
        multiply_qk(0)
        quantise_query(1, 1)
        rotate(0)

        to_transpose = {
            0: [("q", 3, 2)],
            1: [("q", 5, 2)],
            2: [("q", 7, 1), ("w", 1, 0)],
            3: [("w", 1, 1), ("w", 1, 2)],
            4: [("w", 1, 3)],
            6: [("v", 1, 0), ("v", 1, 1)],
            7: [("w", 2, 0), ("w", 2, 1)],
            9: [("w", 2, 2), ("w", 2, 3)],
            11: [("v", 2, 0), ("v", 2, 1)],
            12: [("v", 2, 2), ("v", 2, 3)],
            15: [("w", 3, 0), ("w", 3, 1)],
            17: [("w", 3, 2), ("w", 3, 3)],
            20: [("v", 3, 0), ("v", 3, 1)],
        }
        to_quantise = {
            0: [("q", 2, 1)],
            1: [("q", 3, 2)],
            3: [("q", 5, 2)],
            5: [("q", 7, 1), ("w", 1)],
            8: [("v", 1)],
            11: [("w", 2)],
            14: [("v", 2)],
            20: [("w", 3)],
            23: [("v", 3)],
        }

        last = T_BLOCKS * ROUNDS - 1
        for s in range(last):
            for item in to_transpose.get(s + 1, []):
                if item[0] != "q" and item[1] >= 2:
                    order_words(*item)
            if 1 <= s + 1 <= last:
                multiply_qk(s + 1)
            for item in to_transpose.get(s, []):
                if item[0] == "q":
                    transpose_query(item[1], item[2], scalar_copy)
                else:
                    transpose_rows(item[0], item[1], item[2], scalar_copy)
            if s == 0:
                cos_table(slice(2, 4))
                sin_table(slice(2, 4))
            if s == 1:
                cos_table(slice(4, T_BLOCKS))
                sin_table(slice(4, T_BLOCKS))
            if s >= 1:
                rotate(s)
            if s in (6, 9, 12, 15, 18, 21, 24, 27,):
                add(s, nc.gpsimd)
            for b in {1: [0], 3: [2], 5: [4], 8: [7], 11: [10], 14: [13], 17: [16], 20: [19], 23: [22], 26: [25], 29: [28]}.get(s, []):
                add(b, nc.vector)
            for item in to_quantise.get(s, []):
                if item[0] == "q":
                    quantise_query(item[1], item[2])
                else:
                    quantise_rows(*item)
            if s in (1, 3, 5, 8, 11, 14, 17, 20, 23, 26, 29,):
                add(s, nc.gpsimd)
            r, i = divmod(s, T_BLOCKS)
            for v_block in v_blocks(r, i):
                project_v(r, v_block, tp_pool, "tp")

        half = QK_HEADS // 2
        rotate(last, 0, half)
        add(last - 1, nc.vector)
        rotate(last, half, half)
        add(last, nc.vector, 0, half)
        add(last, nc.vector, half, half)
